import numpy as np
import ml_dtypes


def mxq(x, axis, fmt="e4m3"):
    dtype, down = {"e4m3": (ml_dtypes.float8_e4m3fn, 7), "e5m2": (ml_dtypes.float8_e5m2, 14)}[fmt]
    v = np.moveaxis(np.asarray(x, np.float32).astype(ml_dtypes.bfloat16).astype(np.float64), axis, -1)
    blocks = v.reshape(v.shape[:-1] + (-1, 32))
    amax = np.abs(blocks).max(-1, keepdims=True)
    byte = np.maximum(np.where(amax > 0, np.frexp(amax)[1] - 1 + 127, 0) - down, 1)
    scale = np.exp2(byte - 127.0)
    codes = (blocks / scale).astype(np.float32).astype(dtype).astype(np.float64)
    return np.moveaxis((codes * scale).reshape(v.shape), -1, axis)


WIDE = False


def mx_kscale(k):
    if not WIDE:
        return np.ones(k)
    levels = np.array([30, -30])
    if k % 512:
        return np.exp2(np.random.permutation(np.resize(levels, k // 32))).repeat(32)
    a = np.empty((k // 512, 16))
    for p in range(k // 512):
        a[p, :8] = np.random.permutation(np.resize(levels, 8))
        for g in range(8):
            far = levels[np.abs(levels - a[p, g]) >= 10]
            a[p, g + 8] = far[np.random.randint(len(far))]
    return np.exp2(a.ravel()).repeat(32)


BF16 = ml_dtypes.bfloat16


def bf(x):
    return np.asarray(x, np.float32).astype(BF16)


def f64(x):
    return np.asarray(x).astype(np.float64)


B, L, E, H, DH, RK, RD, MAXLEN = 4, 128, 2048, 16, 128, 512, 128, 4096


def apply_rope(x, cos, sin):
    cos = cos[None, :, None, :]
    sin = sin[None, :, None, :]
    x1, x2 = x[..., 0::2], x[..., 1::2]
    out_real = x1 * cos - x2 * sin
    out_imag = x1 * sin + x2 * cos
    return np.stack([out_real, out_imag], axis=-1).reshape(x.shape)


def setup_inputs():
    s = mx_kscale(E)
    return {"x": bf(np.random.standard_normal((B, L, E)) * s),
            "cos": bf(np.random.uniform(size=(L, RD // 2))),
            "sin": bf(np.random.uniform(size=(L, RD // 2))),
            "wq": bf(np.random.standard_normal((E, H * (DH + RD))) / np.sqrt(E) / s[:, None])}


def reference(x, cos, sin, wq):
    q_all = (mxq(f64(x), 2, "e5m2") @ mxq(f64(wq), 0, "e5m2")).reshape(B, L, H, DH + RD)
    q_head, q_rope = q_all[..., :DH], q_all[..., DH:]
    q_rope = apply_rope(q_rope, f64(cos), f64(sin))
    return np.concatenate([q_head, q_rope], axis=-1)

@@ -1,0 +1,271 @@
+from contextlib import ExitStack
+
+import concourse.mybir as mybir
+from concourse.masks import make_identity
+
+F32 = mybir.dt.float32
+BF16 = mybir.dt.bfloat16
+U32 = mybir.dt.uint32
+U8 = mybir.dt.uint8
+E5X4 = mybir.dt.float8_e5m2_x4
+ALU = mybir.AluOpType
+
+P = 128
+TOKENS, E, NOUT = 512, 2048, 4096
+FLOPS = 2 * TOKENS * E * NOUT
+NPASS = 4
+MT = 4
+GROUPS = 4
+GW = 1024
+ROPE, CONTENT = 1, 0
+
+RAWBUFS = 9
+LS = 5
+GRPBUFS = LS + 2
+WCBUFS = 10
+ADD_ON_G = False
+ACCBANKS = 8
+S_HEADS = [2, 2, 2, 2, 2, 2, 2, 2] + [3, 3, 3, 2, 3, 3, 3, 2] * 3
+ROPE_LAG = 2
+CONTENT_LAG = 1
+
+
+def tile_multiheadlatentattention_pb_kernel(tc, x, cos, sin, wq, out):
+    nc = tc.nc
+    x_rows = x.flatten_outer_dims()
+    out_rows = out.rearrange("b l h d -> (b l) (h d)")
+
+    with ExitStack() as ctx:
+        const = ctx.enter_context(tc.tile_pool(name="const", bufs=1))
+        rawp = ctx.enter_context(tc.tile_pool(name="rawp", bufs=RAWBUFS))
+        xin = ctx.enter_context(tc.tile_pool(name="xin", bufs=4))
+        xgp = ctx.enter_context(tc.tile_pool(name="xgp", bufs=4))
+        grpp = ctx.enter_context(tc.tile_pool(name="grpp", bufs=GRPBUFS))
+        wcp = ctx.enter_context(tc.tile_pool(name="wcp", bufs=WCBUFS))
+        rp = ctx.enter_context(tc.tile_pool(name="rp", bufs=4))
+        otp = ctx.enter_context(tc.tile_pool(name="otp", bufs=8))
+        accp = ctx.enter_context(tc.psum_pool(name="accp", bufs=1))
+        ctx.enter_context(tc.manual_schedule())
+
+        ident = const.tile([P, P], F32, name="ident")
+        cos_sb = const.tile([P, 64], BF16, name="cos_sb")
+        sin_sb = const.tile([P, 64], BF16, name="sin_sb")
+        ctab = const.tile([P, 512], F32, name="ctab")
+        stab = const.tile([P, 512], F32, name="stab")
+        warm = const.tile([P, 8], F32, name="warm")
+        warm2 = const.tile([P, 8], F32, name="warm2")
+        xcodes = const.tile([P, MT, 512], U32, name="xcodes", align_bytes=64)
+        xscales = const.tile([P, MT, 512], U8, name="xscales", align_bytes=64)
+
+        raw, xs, grp, wcodes, wscales, acc, ot = {}, {}, {}, {}, {}, {}, {}
+        nacc = [0]
+
+        def load_raw(s):
+            G, g = s // NPASS, s % NPASS
+            t = rawp.tile([P, 4, GW], BF16, name="raw")
+            raw[(G, g)] = t
+            nc.sync.dma_start(
+                out=t[:],
+                in_=wq[512 * g : 512 * (g + 1), GW * G : GW * (G + 1)].rearrange("(p j) w -> p j w", j=4),
+            )
+
+        def load_x(m):
+            t = xin.tile([P, E], BF16, name="xs")
+            xs[m] = t
+            nc.sync.dma_start(out=t[:], in_=x_rows[P * m : P * (m + 1), :])
+
+        xg = {}
+
+        def x_turn(m):
+            words = xs[m][:].bitcast(F32)
+            t = xgp.tile([P, E], BF16, name="xg", align_bytes=64)
+            xg[m] = t
+            xgw = t[:].bitcast(F32).rearrange("p (g r u) -> p g r u", g=NPASS, u=2)
+            for half in range(2):
+                tp = accp.tile([P, 4, P], F32, name="acc%d" % (nacc[0] % ACCBANKS))
+                nacc[0] += 1
+                for gg in range(2):
+                    g = 2 * half + gg
+                    for u in range(2):
+                        nc.tensor.transpose(tp[:, 2 * gg + u, :], words[:, 256 * g + u : 256 * (g + 1) : 2], ident[:])
+                nc.scalar.copy(
+                    out=xgw[:, 2 * half : 2 * half + 2],
+                    in_=tp[:].rearrange("p (g u) r -> p g r u", u=2),
+                )
+
+        def x_quant(m):
+            nc.vector.quantize_mx(out=xcodes[:, m, :].bitcast(E5X4), scales=xscales[:, m, :], in_=xg[m][:])
+
+        def il_views(u):
+            G, kind, g = u
+            dst = grp[u][:].rearrange("p (h c j) -> p h c j", h=4, j=4)
+            src = raw[(G, g)][:].rearrange("p j (h k c) -> p k h c j", k=2, c=128)[:, kind]
+            return dst, src
+
+        def il_scalar(u, hs):
+            t = grpp.tile([P, 2048], BF16, name="grp", align_bytes=64)
+            grp[u] = t
+            dst, src = il_views(u)
+            if hs > 0:
+                nc.scalar.copy(out=dst[:, 0:hs], in_=src[:, 0:hs])
+
+        def il_vector(u, hs):
+            dst, src = il_views(u)
+            if hs < 4:
+                nc.vector.tensor_copy(out=dst[:, hs:4], in_=src[:, hs:4])
+
+        def quant(u):
+            c = wcp.tile([P, 512], U32, name="wc", align_bytes=64)
+            s = wcp.tile([P, 512], U8, name="ws", align_bytes=64)
+            wcodes[u], wscales[u] = c, s
+            nc.vector.quantize_mx(out=c[:].bitcast(E5X4), scales=s[:], in_=grp[u][:])
+
+        def passes(u):
+            G, kind, g = u
+            for m in range(MT):
+                if g == 0:
+                    a = accp.tile([P, 512], F32, name="acc%d" % (nacc[0] % ACCBANKS))
+                    nacc[0] += 1
+                    acc[(G, kind, m)] = a
+                nc.tensor.matmul_mx(
+                    out=acc[(G, kind, m)][:],
+                    lhsT=xcodes[:, m, P * g : P * (g + 1)].bitcast(E5X4),
+                    lhsT_scale=xscales[:, m, P * g : P * (g + 1)],
+                    rhs=wcodes[u][:].bitcast(E5X4),
+                    rhs_scale=wscales[u][:],
+                    start=(g == 0),
+                    stop=(g == NPASS - 1),
+                )
+
+        def ot_part(G, m, kind):
+            return ot[(G, m)][:].rearrange("p (h k c) -> p k h c", k=2, c=128)[:, kind]
+
+        def rope(G):
+            t1s, t2s = {}, {}
+
+            def mul(m):
+                o = otp.tile([P, GW], F32, name="ot")
+                ot[(G, m)] = o
+                a = acc[(G, ROPE, m)]
+                t1 = rp.tile([P, 512], F32, name="t1")
+                t2 = rp.tile([P, 512], F32, name="t2")
+                t1s[m], t2s[m] = t1, t2
+                nc.vector.tensor_tensor(out=t1[:], in0=a[:], in1=ctab[:], op=ALU.mult)
+                nc.vector.tensor_tensor(out=t2[:], in0=a[:], in1=stab[:], op=ALU.mult)
+
+            def add(m):
+                eng = nc.gpsimd if ADD_ON_G else nc.vector
+                eng.tensor_tensor(
+                    out=ot_part(G, m, ROPE).rearrange("p h (j e) -> p h j e", e=2),
+                    in0=t1s[m][:].rearrange("p (h j e) -> p h j e", h=4, e=2),
+                    in1=t2s[m][:].rearrange("p (h j e) -> p h j e", h=4, e=2)[:, :, :, ::-1],
+                    op=ALU.add,
+                )
+
+            mul(0)
+            for m in range(1, MT):
+                mul(m)
+                add(m - 1)
+            add(MT - 1)
+
+        def content(G):
+            for m in range(MT):
+                if G == GROUPS - 1 and m % 2 == 1:
+                    nc.vector.tensor_copy(
+                        out=ot_part(G, m, CONTENT),
+                        in_=acc[(G, CONTENT, m)][:].rearrange("p (h c) -> p h c", c=128),
+                    )
+                else:
+                    nc.scalar.copy(
+                        out=ot_part(G, m, CONTENT),
+                        in_=acc[(G, CONTENT, m)][:].rearrange("p (h c) -> p h c", c=128),
+                    )
+                nc.sync.dma_start(out=out_rows[P * m : P * (m + 1), GW * G : GW * (G + 1)], in_=ot[(G, m)][:])
+
+        nc.scalar.dma_start(out=cos_sb[:], in_=cos)
+        nc.scalar.dma_start(out=sin_sb[:], in_=sin)
+        nc.vector.memset(warm[:], 0.0)
+        nc.scalar.copy(out=warm2[:], in_=warm[:])
+        make_identity(nc, ident[:])
+        load_raw(0)
+        load_x(0)
+        load_x(1)
+        load_raw(1)
+        load_x(2)
+        load_x(3)
+        for s in range(2, RAWBUFS):
+            load_raw(s)
+        next_raw = [RAWBUFS]
+
+        cv = ctab[:].rearrange("p (h j e) -> p h j e", h=4, e=2)
+        sv = stab[:].rearrange("p (h j e) -> p h j e", h=4, e=2)
+        for h in range(4):
+            for e in range(2):
+                nc.vector.tensor_copy(out=cv[:, h, :, e], in_=cos_sb[:])
+                nc.vector.tensor_scalar_mul(out=sv[:, h, :, e], in0=sin_sb[:], scalar1=(1.0 if e == 0 else -1.0))
+
+        prep = []
+        for g in range(NPASS):
+            prep.append((0, ROPE, g))
+            prep.append((0, CONTENT, g))
+        for G in range(1, GROUPS):
+            for kind in (ROPE, CONTENT):
+                for g in range(NPASS):
+                    prep.append((G, kind, g))
+        pe_order = []
+        for G in range(GROUPS):
+            for kind in (ROPE, CONTENT):
+                for g in range(NPASS):
+                    pe_order.append((G, kind, g))
+
+        uses = {}
+        quanted = set()
+        pe_ptr = 0
+        pending = []
+        evacuated = set()
+        n = len(prep)
+        for t in range(-LS, n + 4):
+            a = t + LS
+            if 0 <= a < n:
+                il_scalar(prep[a], S_HEADS[a % len(S_HEADS)])
+            if a == 1:
+                x_turn(0)
+                x_turn(1)
+            if a == 3:
+                x_turn(2)
+                x_turn(3)
+            if t == 2:
+                x_quant(0)
+                x_quant(1)
+            if t == 4:
+                x_quant(2)
+                x_quant(3)
+            if 0 <= t < n:
+                u = prep[t]
+                il_vector(u, S_HEADS[t % len(S_HEADS)])
+                key = (u[0], u[2])
+                uses[key] = uses.get(key, 0) + 1
+                if uses[key] == 2 and next_raw[0] < GROUPS * NPASS:
+                    load_raw(next_raw[0])
+                    next_raw[0] += 1
+            if 1 <= t <= n:
+                quant(prep[t - 1])
+                quanted.add(prep[t - 1])
+            for job in [j for j in pending if j[0] <= t]:
+                pending.remove(job)
+                evacuated.add((job[2], job[1]))
+                if job[1] == ROPE:
+                    rope(job[2])
+                else:
+                    content(job[2])
+            if t >= 4:
+                while pe_ptr < n and pe_order[pe_ptr] in quanted:
+                    u = pe_order[pe_ptr]
+                    if u[2] == 0 and pe_ptr >= 2 * NPASS:
+                        prev = pe_order[pe_ptr - 1 - NPASS]
+                        if (prev[0], prev[1]) not in evacuated:
+                            break
+                    passes(u)
+                    pe_ptr += 1
+                    if u[2] == NPASS - 1:
+                        pending.append((t + (ROPE_LAG if u[1] == ROPE else CONTENT_LAG), u[1], u[0]))

@@ -19,14 +19,17 @@ GROUPS = 4
 GW = 1024
 ROPE, CONTENT = 1, 0
 
-RAWBUFS = 9
-LS = 5
+RAWBUFS = 8
+OTBUFS = 8
+SLAB_MAJOR = 3
+LS = 3
 GRPBUFS = LS + 2
 WCBUFS = 10
-ADD_ON_G = False
+G_ADDS = 2
+X_COPY_ON_V = [0, 0, 0, 0, 0, 0, 0, 0]
 ACCBANKS = 8
-S_HEADS = [2, 2, 2, 2, 2, 2, 2, 2] + [3, 3, 3, 2, 3, 3, 3, 2] * 3
-ROPE_LAG = 2
+S_HEADS = [1,1,1,1,1,3,2,1,4,3,1,2,2,1,2,2,4,3,2,3,3,2,3,3,2,4,3,2,4,3,2,4]
+ROPE_LAG = 1
 CONTENT_LAG = 1
 
 
@@ -43,7 +46,8 @@ def tile_multiheadlatentattention_pb_kernel(tc, x, cos, sin, wq, out):
         grpp = ctx.enter_context(tc.tile_pool(name="grpp", bufs=GRPBUFS))
         wcp = ctx.enter_context(tc.tile_pool(name="wcp", bufs=WCBUFS))
         rp = ctx.enter_context(tc.tile_pool(name="rp", bufs=4))
-        otp = ctx.enter_context(tc.tile_pool(name="otp", bufs=8))
+        otp = ctx.enter_context(tc.tile_pool(name="otp", bufs=OTBUFS))
+        otl = ctx.enter_context(tc.tile_pool(name="otl", bufs=8))
         accp = ctx.enter_context(tc.psum_pool(name="accp", bufs=1))
         ctx.enter_context(tc.manual_schedule())
 
@@ -88,10 +92,16 @@ def tile_multiheadlatentattention_pb_kernel(tc, x, cos, sin, wq, out):
                     g = 2 * half + gg
                     for u in range(2):
                         nc.tensor.transpose(tp[:, 2 * gg + u, :], words[:, 256 * g + u : 256 * (g + 1) : 2], ident[:])
-                nc.scalar.copy(
-                    out=xgw[:, 2 * half : 2 * half + 2],
-                    in_=tp[:].rearrange("p (g u) r -> p g r u", u=2),
-                )
+                if X_COPY_ON_V[2 * m + half]:
+                    nc.vector.tensor_copy(
+                        out=xgw[:, 2 * half : 2 * half + 2],
+                        in_=tp[:].rearrange("p (g u) r -> p g r u", u=2),
+                    )
+                else:
+                    nc.scalar.copy(
+                        out=xgw[:, 2 * half : 2 * half + 2],
+                        in_=tp[:].rearrange("p (g u) r -> p g r u", u=2),
+                    )
 
         def x_quant(m):
             nc.vector.quantize_mx(out=xcodes[:, m, :].bitcast(E5X4), scales=xscales[:, m, :], in_=xg[m][:])
@@ -111,7 +121,10 @@ def tile_multiheadlatentattention_pb_kernel(tc, x, cos, sin, wq, out):
 
         def il_vector(u, hs):
             dst, src = il_views(u)
-            if hs < 4:
+            if hs == 1:
+                nc.vector.tensor_copy(out=dst[:, 1:3], in_=src[:, 1:3])
+                nc.vector.tensor_copy(out=dst[:, 3:4], in_=src[:, 3:4])
+            elif hs < 4:
                 nc.vector.tensor_copy(out=dst[:, hs:4], in_=src[:, hs:4])
 
         def quant(u):
@@ -124,8 +137,7 @@ def tile_multiheadlatentattention_pb_kernel(tc, x, cos, sin, wq, out):
             G, kind, g = u
             for m in range(MT):
                 if g == 0:
-                    a = accp.tile([P, 512], F32, name="acc%d" % (nacc[0] % ACCBANKS))
-                    nacc[0] += 1
+                    a = accp.tile([P, 512], F32, name="acc%d" % (4 * kind + m))
                     acc[(G, kind, m)] = a
                 nc.tensor.matmul_mx(
                     out=acc[(G, kind, m)][:],
@@ -138,14 +150,28 @@ def tile_multiheadlatentattention_pb_kernel(tc, x, cos, sin, wq, out):
                 )
 
         def ot_part(G, m, kind):
+            if G == GROUPS - 1:
+                return ot[(G, m, kind)][:].rearrange("p (h c) -> p h c", c=128)
             return ot[(G, m)][:].rearrange("p (h k c) -> p k h c", k=2, c=128)[:, kind]
+
+        def store_part(G, m, kind):
+            nc.sync.dma_start(
+                out=out_rows[P * m : P * (m + 1), GW * G : GW * (G + 1)].rearrange("p (h k c) -> p k h c", k=2, c=128)[:, kind],
+                in_=ot_part(G, m, kind),
+            )
 
         def rope(G):
             t1s, t2s = {}, {}
 
             def mul(m):
-                o = otp.tile([P, GW], F32, name="ot")
-                ot[(G, m)] = o
+                if G == GROUPS - 1:
+                    o = otl.tile([P, 512], F32, name="otl")
+                    ot[(G, m, ROPE)] = o
+                    o = otl.tile([P, 512], F32, name="otl")
+                    ot[(G, m, CONTENT)] = o
+                else:
+                    o = otp.tile([P, GW], F32, name="ot")
+                    ot[(G, m)] = o
                 a = acc[(G, ROPE, m)]
                 t1 = rp.tile([P, 512], F32, name="t1")
                 t2 = rp.tile([P, 512], F32, name="t2")
@@ -154,13 +180,15 @@ def tile_multiheadlatentattention_pb_kernel(tc, x, cos, sin, wq, out):
                 nc.vector.tensor_tensor(out=t2[:], in0=a[:], in1=stab[:], op=ALU.mult)
 
             def add(m):
-                eng = nc.gpsimd if ADD_ON_G else nc.vector
+                eng = nc.gpsimd if m < G_ADDS else nc.vector
                 eng.tensor_tensor(
                     out=ot_part(G, m, ROPE).rearrange("p h (j e) -> p h j e", e=2),
                     in0=t1s[m][:].rearrange("p (h j e) -> p h j e", h=4, e=2),
                     in1=t2s[m][:].rearrange("p (h j e) -> p h j e", h=4, e=2)[:, :, :, ::-1],
                     op=ALU.add,
                 )
+                if G == GROUPS - 1:
+                    store_part(G, m, ROPE)
 
             mul(0)
             for m in range(1, MT):
@@ -180,7 +208,10 @@ def tile_multiheadlatentattention_pb_kernel(tc, x, cos, sin, wq, out):
                         out=ot_part(G, m, CONTENT),
                         in_=acc[(G, CONTENT, m)][:].rearrange("p (h c) -> p h c", c=128),
                     )
-                nc.sync.dma_start(out=out_rows[P * m : P * (m + 1), GW * G : GW * (G + 1)], in_=ot[(G, m)][:])
+                if G == GROUPS - 1:
+                    store_part(G, m, CONTENT)
+                else:
+                    nc.sync.dma_start(out=out_rows[P * m : P * (m + 1), GW * G : GW * (G + 1)], in_=ot[(G, m)][:])
 
         nc.scalar.dma_start(out=cos_sb[:], in_=cos)
         nc.scalar.dma_start(out=sin_sb[:], in_=sin)
@@ -205,18 +236,16 @@ def tile_multiheadlatentattention_pb_kernel(tc, x, cos, sin, wq, out):
                 nc.vector.tensor_scalar_mul(out=sv[:, h, :, e], in0=sin_sb[:], scalar1=(1.0 if e == 0 else -1.0))
 
         prep = []
-        for g in range(NPASS):
-            prep.append((0, ROPE, g))
-            prep.append((0, CONTENT, g))
-        for G in range(1, GROUPS):
-            for kind in (ROPE, CONTENT):
-                for g in range(NPASS):
-                    prep.append((G, kind, g))
-        pe_order = []
         for G in range(GROUPS):
-            for kind in (ROPE, CONTENT):
+            if G < SLAB_MAJOR:
                 for g in range(NPASS):
-                    pe_order.append((G, kind, g))
+                    prep.append((G, ROPE, g))
+                    prep.append((G, CONTENT, g))
+            else:
+                for kind in (ROPE, CONTENT):
+                    for g in range(NPASS):
+                        prep.append((G, kind, g))
+        pe_order = prep
 
         uses = {}
         quanted = set()
@@ -261,10 +290,8 @@ def tile_multiheadlatentattention_pb_kernel(tc, x, cos, sin, wq, out):
             if t >= 4:
                 while pe_ptr < n and pe_order[pe_ptr] in quanted:
                     u = pe_order[pe_ptr]
-                    if u[2] == 0 and pe_ptr >= 2 * NPASS:
-                        prev = pe_order[pe_ptr - 1 - NPASS]
-                        if (prev[0], prev[1]) not in evacuated:
-                            break
+                    if u[2] == 0 and u[0] > 0 and (u[0] - 1, u[1]) not in evacuated:
+                        break
                     passes(u)
                     pe_ptr += 1
                     if u[2] == NPASS - 1:

@@ -20,17 +20,14 @@ GW = 1024
 ROPE, CONTENT = 1, 0
 
 RAWBUFS = 8
-OTBUFS = 8
-SLAB_MAJOR = 3
-LS = 3
-GRPBUFS = LS + 2
-WCBUFS = 10
+LS = 0
+GRPBUFS = LS + 3
+WCBUFS = 6
 G_ADDS = 2
-X_COPY_ON_V = [0, 0, 0, 0, 0, 0, 0, 0]
-ACCBANKS = 8
-S_HEADS = [1,1,1,1,1,3,2,1,4,3,1,2,2,1,2,2,4,3,2,3,3,2,3,3,2,4,3,2,4,3,2,4]
+MERGE_MUL = True
 ROPE_LAG = 1
-CONTENT_LAG = 1
+CONTENT_LAG = 2
+S_HEADS = [2,0,0,2,2,3,1,2,4,2,1,2,3,2,0,3,4,2,2,4,3,2,1,2,4,3,4,2,4,4,3,2]
 
 
 def tile_multiheadlatentattention_pb_kernel(tc, x, cos, sin, wq, out):
@@ -41,28 +38,26 @@ def tile_multiheadlatentattention_pb_kernel(tc, x, cos, sin, wq, out):
     with ExitStack() as ctx:
         const = ctx.enter_context(tc.tile_pool(name="const", bufs=1))
         rawp = ctx.enter_context(tc.tile_pool(name="rawp", bufs=RAWBUFS))
-        xin = ctx.enter_context(tc.tile_pool(name="xin", bufs=4))
-        xgp = ctx.enter_context(tc.tile_pool(name="xgp", bufs=4))
+        k4p = ctx.enter_context(tc.tile_pool(name="k4p", bufs=8))
         grpp = ctx.enter_context(tc.tile_pool(name="grpp", bufs=GRPBUFS))
         wcp = ctx.enter_context(tc.tile_pool(name="wcp", bufs=WCBUFS))
-        rp = ctx.enter_context(tc.tile_pool(name="rp", bufs=4))
-        otp = ctx.enter_context(tc.tile_pool(name="otp", bufs=OTBUFS))
-        otl = ctx.enter_context(tc.tile_pool(name="otl", bufs=8))
-        accp = ctx.enter_context(tc.psum_pool(name="accp", bufs=1))
+        otp = ctx.enter_context(tc.tile_pool(name="otp", bufs=3))
+        psum = ctx.enter_context(tc.psum_pool(name="psum", bufs=1))
         ctx.enter_context(tc.manual_schedule())
 
         ident = const.tile([P, P], F32, name="ident")
         cos_sb = const.tile([P, 64], BF16, name="cos_sb")
         sin_sb = const.tile([P, 64], BF16, name="sin_sb")
-        ctab = const.tile([P, 512], F32, name="ctab")
-        stab = const.tile([P, 512], F32, name="stab")
+        tab = const.tile([P, 2, 512], F32, name="tab")
         warm = const.tile([P, 8], F32, name="warm")
         warm2 = const.tile([P, 8], F32, name="warm2")
         xcodes = const.tile([P, MT, 512], U32, name="xcodes", align_bytes=64)
         xscales = const.tile([P, MT, 512], U8, name="xscales", align_bytes=64)
 
-        raw, xs, grp, wcodes, wscales, acc, ot = {}, {}, {}, {}, {}, {}, {}
-        nacc = [0]
+        raw, xs, xg, grp, wcodes, wscales, acc, ot = {}, {}, {}, {}, {}, {}, {}, {}
+
+        def bank(i, shape):
+            return psum.tile(shape, F32, name="bank%d" % i)
 
         def load_raw(s):
             G, g = s // NPASS, s % NPASS
@@ -74,121 +69,128 @@ def tile_multiheadlatentattention_pb_kernel(tc, x, cos, sin, wq, out):
             )
 
         def load_x(m):
-            t = xin.tile([P, E], BF16, name="xs")
+            t = k4p.tile([P, E], BF16, name="k4", align_bytes=64)
             xs[m] = t
             nc.sync.dma_start(out=t[:], in_=x_rows[P * m : P * (m + 1), :])
 
-        xg = {}
-
         def x_turn(m):
             words = xs[m][:].bitcast(F32)
-            t = xgp.tile([P, E], BF16, name="xg", align_bytes=64)
+            t = k4p.tile([P, E], BF16, name="k4", align_bytes=64)
             xg[m] = t
             xgw = t[:].bitcast(F32).rearrange("p (g r u) -> p g r u", g=NPASS, u=2)
             for half in range(2):
-                tp = accp.tile([P, 4, P], F32, name="acc%d" % (nacc[0] % ACCBANKS))
-                nacc[0] += 1
+                tp = bank(2 * m + half, [P, 4, P])
                 for gg in range(2):
                     g = 2 * half + gg
                     for u in range(2):
                         nc.tensor.transpose(tp[:, 2 * gg + u, :], words[:, 256 * g + u : 256 * (g + 1) : 2], ident[:])
-                if X_COPY_ON_V[2 * m + half]:
-                    nc.vector.tensor_copy(
-                        out=xgw[:, 2 * half : 2 * half + 2],
-                        in_=tp[:].rearrange("p (g u) r -> p g r u", u=2),
-                    )
-                else:
-                    nc.scalar.copy(
-                        out=xgw[:, 2 * half : 2 * half + 2],
-                        in_=tp[:].rearrange("p (g u) r -> p g r u", u=2),
-                    )
+                nc.scalar.copy(
+                    out=xgw[:, 2 * half : 2 * half + 2],
+                    in_=tp[:].rearrange("p (g u) r -> p g r u", u=2),
+                )
 
         def x_quant(m):
             nc.vector.quantize_mx(out=xcodes[:, m, :].bitcast(E5X4), scales=xscales[:, m, :], in_=xg[m][:])
 
         def il_views(u):
             G, kind, g = u
-            dst = grp[u][:].rearrange("p (h c j) -> p h c j", h=4, j=4)
+            dst = grp[u].rearrange("p (h c j) -> p h c j", h=4, j=4)
             src = raw[(G, g)][:].rearrange("p j (h k c) -> p k h c j", k=2, c=128)[:, kind]
             return dst, src
 
-        def il_scalar(u, hs):
-            t = grpp.tile([P, 2048], BF16, name="grp", align_bytes=64)
-            grp[u] = t
-            dst, src = il_views(u)
-            if hs > 0:
-                nc.scalar.copy(out=dst[:, 0:hs], in_=src[:, 0:hs])
+        def il_scalar(units, heads):
+            t = grpp.tile([P, 2, 2048], BF16, name="grp", align_bytes=64)
+            for i in range(len(units)):
+                grp[units[i]] = t[:, i, :]
+            grp[tuple(units)] = t
+            for i in range(len(units)):
+                dst, src = il_views(units[i])
+                if heads[i] > 0:
+                    nc.scalar.copy(out=dst[:, 0 : heads[i]], in_=src[:, 0 : heads[i]])
 
-        def il_vector(u, hs):
-            dst, src = il_views(u)
-            if hs == 1:
-                nc.vector.tensor_copy(out=dst[:, 1:3], in_=src[:, 1:3])
-                nc.vector.tensor_copy(out=dst[:, 3:4], in_=src[:, 3:4])
-            elif hs < 4:
-                nc.vector.tensor_copy(out=dst[:, hs:4], in_=src[:, hs:4])
+        def il_vector(units, heads):
+            for i in range(len(units)):
+                dst, src = il_views(units[i])
+                lo = heads[i]
+                if lo == 1:
+                    nc.vector.tensor_copy(out=dst[:, 1:3], in_=src[:, 1:3])
+                    nc.vector.tensor_copy(out=dst[:, 3:4], in_=src[:, 3:4])
+                elif lo < 4:
+                    nc.vector.tensor_copy(out=dst[:, lo:4], in_=src[:, lo:4])
 
-        def quant(u):
-            c = wcp.tile([P, 512], U32, name="wc", align_bytes=64)
-            s = wcp.tile([P, 512], U8, name="ws", align_bytes=64)
-            wcodes[u], wscales[u] = c, s
-            nc.vector.quantize_mx(out=c[:].bitcast(E5X4), scales=s[:], in_=grp[u][:])
+        def quant(units):
+            n = len(units)
+            c = wcp.tile([P, 2, 512], U32, name="wc", align_bytes=64)
+            s = wcp.tile([P, 2, 512], U8, name="ws", align_bytes=64)
+            for i in range(n):
+                wcodes[units[i]], wscales[units[i]] = c[:, i, :], s[:, i, :]
+            t = grp[tuple(units)]
+            nc.vector.quantize_mx(
+                out=c[:, 0:n, :].rearrange("p a w -> p (a w)").bitcast(E5X4),
+                scales=s[:, 0:n, :].rearrange("p a w -> p (a w)"),
+                in_=t[:, 0:n, :].rearrange("p a w -> p (a w)"),
+            )
 
         def passes(u):
             G, kind, g = u
             for m in range(MT):
                 if g == 0:
-                    a = accp.tile([P, 512], F32, name="acc%d" % (4 * kind + m))
+                    a = bank(4 * kind + m, [P, 512])
                     acc[(G, kind, m)] = a
                 nc.tensor.matmul_mx(
                     out=acc[(G, kind, m)][:],
                     lhsT=xcodes[:, m, P * g : P * (g + 1)].bitcast(E5X4),
                     lhsT_scale=xscales[:, m, P * g : P * (g + 1)],
-                    rhs=wcodes[u][:].bitcast(E5X4),
-                    rhs_scale=wscales[u][:],
+                    rhs=wcodes[u].bitcast(E5X4),
+                    rhs_scale=wscales[u],
                     start=(g == 0),
                     stop=(g == NPASS - 1),
                 )
 
-        def ot_part(G, m, kind):
+        def ot_part(G, kind):
             if G == GROUPS - 1:
-                return ot[(G, m, kind)][:].rearrange("p (h c) -> p h c", c=128)
-            return ot[(G, m)][:].rearrange("p (h k c) -> p k h c", k=2, c=128)[:, kind]
+                return ot[G][:, kind].rearrange("p m (h c) -> p m h c", c=128)
+            return ot[G][:].rearrange("p m (h k c) -> p k m h c", k=2, c=128)[:, kind]
 
-        def store_part(G, m, kind):
-            nc.sync.dma_start(
-                out=out_rows[P * m : P * (m + 1), GW * G : GW * (G + 1)].rearrange("p (h k c) -> p k h c", k=2, c=128)[:, kind],
-                in_=ot_part(G, m, kind),
-            )
+        def store(G, m, kind):
+            rows = out_rows[P * m : P * (m + 1), GW * G : GW * (G + 1)]
+            if G == GROUPS - 1:
+                nc.sync.dma_start(
+                    out=rows.rearrange("p (h k c) -> p k h c", k=2, c=128)[:, kind],
+                    in_=ot[G][:, kind, m, :].rearrange("p (h c) -> p h c", c=128),
+                )
+            elif kind == CONTENT:
+                nc.sync.dma_start(out=rows, in_=ot[G][:, m, :])
 
         def rope(G):
-            t1s, t2s = {}, {}
+            if G == GROUPS - 1:
+                o = otp.tile([P, 2, MT, 512], F32, name="ot")
+            else:
+                o = otp.tile([P, MT, GW], F32, name="ot")
+            ot[G] = o
+            prod = {}
 
             def mul(m):
-                if G == GROUPS - 1:
-                    o = otl.tile([P, 512], F32, name="otl")
-                    ot[(G, m, ROPE)] = o
-                    o = otl.tile([P, 512], F32, name="otl")
-                    ot[(G, m, CONTENT)] = o
-                else:
-                    o = otp.tile([P, GW], F32, name="ot")
-                    ot[(G, m)] = o
                 a = acc[(G, ROPE, m)]
-                t1 = rp.tile([P, 512], F32, name="t1")
-                t2 = rp.tile([P, 512], F32, name="t2")
-                t1s[m], t2s[m] = t1, t2
-                nc.vector.tensor_tensor(out=t1[:], in0=a[:], in1=ctab[:], op=ALU.mult)
-                nc.vector.tensor_tensor(out=t2[:], in0=a[:], in1=stab[:], op=ALU.mult)
+                t = k4p.tile([P, 2, 512], F32, name="k4", align_bytes=64)
+                prod[m] = t
+                if MERGE_MUL:
+                    nc.vector.tensor_tensor(
+                        out=t[:], in0=tab[:], in1=a[:].rearrange("p (o n) -> p o n", o=1).to_broadcast([P, 2, 512]), op=ALU.mult
+                    )
+                else:
+                    nc.vector.tensor_tensor(out=t[:, 0, :], in0=tab[:, 0, :], in1=a[:], op=ALU.mult)
+                    nc.vector.tensor_tensor(out=t[:, 1, :], in0=tab[:, 1, :], in1=a[:], op=ALU.mult)
 
             def add(m):
                 eng = nc.gpsimd if m < G_ADDS else nc.vector
                 eng.tensor_tensor(
-                    out=ot_part(G, m, ROPE).rearrange("p h (j e) -> p h j e", e=2),
-                    in0=t1s[m][:].rearrange("p (h j e) -> p h j e", h=4, e=2),
-                    in1=t2s[m][:].rearrange("p (h j e) -> p h j e", h=4, e=2)[:, :, :, ::-1],
+                    out=ot_part(G, ROPE)[:, m].rearrange("p h (j e) -> p h j e", e=2),
+                    in0=prod[m][:, 0, :].rearrange("p (h j e) -> p h j e", h=4, e=2),
+                    in1=prod[m][:, 1, :].rearrange("p (h j e) -> p h j e", h=4, e=2)[:, :, :, ::-1],
                     op=ALU.add,
                 )
-                if G == GROUPS - 1:
-                    store_part(G, m, ROPE)
+                store(G, m, ROPE)
 
             mul(0)
             for m in range(1, MT):
@@ -198,20 +200,12 @@ def tile_multiheadlatentattention_pb_kernel(tc, x, cos, sin, wq, out):
 
         def content(G):
             for m in range(MT):
+                src = acc[(G, CONTENT, m)][:].rearrange("p (h c) -> p h c", c=128)
                 if G == GROUPS - 1 and m % 2 == 1:
-                    nc.vector.tensor_copy(
-                        out=ot_part(G, m, CONTENT),
-                        in_=acc[(G, CONTENT, m)][:].rearrange("p (h c) -> p h c", c=128),
-                    )
+                    nc.vector.tensor_copy(out=ot_part(G, CONTENT)[:, m], in_=src)
                 else:
-                    nc.scalar.copy(
-                        out=ot_part(G, m, CONTENT),
-                        in_=acc[(G, CONTENT, m)][:].rearrange("p (h c) -> p h c", c=128),
-                    )
-                if G == GROUPS - 1:
-                    store_part(G, m, CONTENT)
-                else:
-                    nc.sync.dma_start(out=out_rows[P * m : P * (m + 1), GW * G : GW * (G + 1)], in_=ot[(G, m)][:])
+                    nc.scalar.copy(out=ot_part(G, CONTENT)[:, m], in_=src)
+                store(G, m, CONTENT)
 
         nc.scalar.dma_start(out=cos_sb[:], in_=cos)
         nc.scalar.dma_start(out=sin_sb[:], in_=sin)
@@ -228,16 +222,15 @@ def tile_multiheadlatentattention_pb_kernel(tc, x, cos, sin, wq, out):
             load_raw(s)
         next_raw = [RAWBUFS]
 
-        cv = ctab[:].rearrange("p (h j e) -> p h j e", h=4, e=2)
-        sv = stab[:].rearrange("p (h j e) -> p h j e", h=4, e=2)
+        tv = tab[:].rearrange("p t (h j e) -> p t h j e", h=4, e=2)
         for h in range(4):
             for e in range(2):
-                nc.vector.tensor_copy(out=cv[:, h, :, e], in_=cos_sb[:])
-                nc.vector.tensor_scalar_mul(out=sv[:, h, :, e], in0=sin_sb[:], scalar1=(1.0 if e == 0 else -1.0))
+                nc.vector.tensor_copy(out=tv[:, 0, h, :, e], in_=cos_sb[:])
+                nc.vector.tensor_scalar_mul(out=tv[:, 1, h, :, e], in0=sin_sb[:], scalar1=(1.0 if e == 0 else -1.0))
 
         prep = []
         for G in range(GROUPS):
-            if G < SLAB_MAJOR:
+            if G < GROUPS - 1:
                 for g in range(NPASS):
                     prep.append((G, ROPE, g))
                     prep.append((G, CONTENT, g))
@@ -245,54 +238,57 @@ def tile_multiheadlatentattention_pb_kernel(tc, x, cos, sin, wq, out):
                 for kind in (ROPE, CONTENT):
                     for g in range(NPASS):
                         prep.append((G, kind, g))
-        pe_order = prep
+        steps = []
+        for i in range(0, len(prep) - 2, 2):
+            steps.append(([prep[i], prep[i + 1]], [S_HEADS[i], S_HEADS[i + 1]]))
+        steps.append(([prep[-2]], [S_HEADS[-2]]))
+        steps.append(([prep[-1]], [S_HEADS[-1]]))
 
         uses = {}
-        quanted = set()
-        pe_ptr = 0
         pending = []
-        evacuated = set()
-        n = len(prep)
-        for t in range(-LS, n + 4):
-            a = t + LS
-            if 0 <= a < n:
-                il_scalar(prep[a], S_HEADS[a % len(S_HEADS)])
-            if a == 1:
-                x_turn(0)
-                x_turn(1)
-            if a == 3:
-                x_turn(2)
-                x_turn(3)
-            if t == 2:
+        done = set()
+        pe_jobs = []
+        n = len(steps)
+        for t in range(-LS - 1, n + 4):
+            if t == 1:
                 x_quant(0)
                 x_quant(1)
-            if t == 4:
+            if t == 2:
                 x_quant(2)
                 x_quant(3)
             if 0 <= t < n:
-                u = prep[t]
-                il_vector(u, S_HEADS[t % len(S_HEADS)])
-                key = (u[0], u[2])
-                uses[key] = uses.get(key, 0) + 1
-                if uses[key] == 2 and next_raw[0] < GROUPS * NPASS:
-                    load_raw(next_raw[0])
-                    next_raw[0] += 1
+                il_vector(steps[t][0], steps[t][1])
+                for u in steps[t][0]:
+                    key = (u[0], u[2])
+                    uses[key] = uses.get(key, 0) + 1
+                    if uses[key] == 2 and next_raw[0] < GROUPS * NPASS:
+                        load_raw(next_raw[0])
+                        next_raw[0] += 1
             if 1 <= t <= n:
-                quant(prep[t - 1])
-                quanted.add(prep[t - 1])
+                quant(steps[t - 1][0])
+                pe_jobs.extend(steps[t - 1][0])
             for job in [j for j in pending if j[0] <= t]:
                 pending.remove(job)
-                evacuated.add((job[2], job[1]))
+                done.add((job[2], job[1]))
                 if job[1] == ROPE:
                     rope(job[2])
                 else:
                     content(job[2])
-            if t >= 4:
-                while pe_ptr < n and pe_order[pe_ptr] in quanted:
-                    u = pe_order[pe_ptr]
-                    if u[2] == 0 and u[0] > 0 and (u[0] - 1, u[1]) not in evacuated:
+            if t >= 2:
+                while len(pe_jobs) > 0:
+                    u = pe_jobs[0]
+                    if u[2] == 0 and u[0] > 0 and (u[0] - 1, u[1]) not in done:
                         break
                     passes(u)
-                    pe_ptr += 1
+                    pe_jobs.pop(0)
                     if u[2] == NPASS - 1:
                         pending.append((t + (ROPE_LAG if u[1] == ROPE else CONTENT_LAG), u[1], u[0]))
+            a = t + LS + 1
+            if 0 <= a < n:
+                il_scalar(steps[a][0], steps[a][1])
+            if a == 0:
+                x_turn(0)
+                x_turn(1)
+            if a == 1:
+                x_turn(2)
+                x_turn(3)

@@ -23,11 +23,12 @@ RAWBUFS = 8
 LS = 0
 GRPBUFS = LS + 3
 WCBUFS = 6
-G_ADDS = 2
+G_ADDS = 3
 MERGE_MUL = True
+IL4 = True
 ROPE_LAG = 1
 CONTENT_LAG = 2
-S_HEADS = [2,0,0,2,2,3,1,2,4,2,1,2,3,2,0,3,4,2,2,4,3,2,1,2,4,3,4,2,4,4,3,2]
+S_HEADS = [1,1,0,2,2,3,1,2,4,2,2,2,3,3,0,3,4,2,2,4,4,2,1,2,4,2,3,3,4,4,3,4]
 
 
 def tile_multiheadlatentattention_pb_kernel(tc, x, cos, sin, wq, out):
@@ -94,8 +95,12 @@ def tile_multiheadlatentattention_pb_kernel(tc, x, cos, sin, wq, out):
 
         def il_views(u):
             G, kind, g = u
-            dst = grp[u].rearrange("p (h c j) -> p h c j", h=4, j=4)
-            src = raw[(G, g)][:].rearrange("p j (h k c) -> p k h c j", k=2, c=128)[:, kind]
+            if IL4:
+                dst = grp[u].rearrange("p (h b i j) -> p h b j i", h=4, i=4, j=4)
+                src = raw[(G, g)][:].rearrange("p j (h k b i) -> p k h b j i", k=2, b=32, i=4)[:, kind]
+            else:
+                dst = grp[u].rearrange("p (h c j) -> p h c j", h=4, j=4)
+                src = raw[(G, g)][:].rearrange("p j (h k c) -> p k h c j", k=2, c=128)[:, kind]
             return dst, src
 
         def il_scalar(units, heads):
@@ -174,20 +179,19 @@ def tile_multiheadlatentattention_pb_kernel(tc, x, cos, sin, wq, out):
                 a = acc[(G, ROPE, m)]
                 t = k4p.tile([P, 2, 512], F32, name="k4", align_bytes=64)
                 prod[m] = t
-                if MERGE_MUL:
-                    nc.vector.tensor_tensor(
-                        out=t[:], in0=tab[:], in1=a[:].rearrange("p (o n) -> p o n", o=1).to_broadcast([P, 2, 512]), op=ALU.mult
-                    )
-                else:
-                    nc.vector.tensor_tensor(out=t[:, 0, :], in0=tab[:, 0, :], in1=a[:], op=ALU.mult)
-                    nc.vector.tensor_tensor(out=t[:, 1, :], in0=tab[:, 1, :], in1=a[:], op=ALU.mult)
+                nc.vector.tensor_tensor(
+                    out=t[:].rearrange("p o (q e) -> p o q e", e=2),
+                    in0=tab[:].rearrange("p o (q e) -> p o q e", e=2),
+                    in1=a[:].rearrange("p (q o z) -> p o q z", o=2, z=1).to_broadcast([P, 2, 256, 2]),
+                    op=ALU.mult,
+                )
 
             def add(m):
                 eng = nc.gpsimd if m < G_ADDS else nc.vector
                 eng.tensor_tensor(
-                    out=ot_part(G, ROPE)[:, m].rearrange("p h (j e) -> p h j e", e=2),
-                    in0=prod[m][:, 0, :].rearrange("p (h j e) -> p h j e", h=4, e=2),
-                    in1=prod[m][:, 1, :].rearrange("p (h j e) -> p h j e", h=4, e=2)[:, :, :, ::-1],
+                    out=ot_part(G, ROPE)[:, m],
+                    in0=prod[m][:, 0, :].rearrange("p (h c) -> p h c", c=128),
+                    in1=prod[m][:, 1, :].rearrange("p (h c) -> p h c", c=128),
                     op=ALU.add,
                 )
                 store(G, m, ROPE)
@@ -225,8 +229,8 @@ def tile_multiheadlatentattention_pb_kernel(tc, x, cos, sin, wq, out):
         tv = tab[:].rearrange("p t (h j e) -> p t h j e", h=4, e=2)
         for h in range(4):
             for e in range(2):
-                nc.vector.tensor_copy(out=tv[:, 0, h, :, e], in_=cos_sb[:])
-                nc.vector.tensor_scalar_mul(out=tv[:, 1, h, :, e], in0=sin_sb[:], scalar1=(1.0 if e == 0 else -1.0))
+                nc.vector.tensor_copy(out=tv[:, e, h, :, e], in_=cos_sb[:])
+                nc.vector.tensor_scalar_mul(out=tv[:, e, h, :, 1 - e], in0=sin_sb[:], scalar1=(1.0 if e == 0 else -1.0))
 
         prep = []
         for G in range(GROUPS):

@@ -200,7 +200,7 @@ def tile_multiheadlatentattention_pb_kernel(tc, x, cos, sin, wq, out):
             for m in range(1, MT):
                 mul(m)
                 add(m - 1)
-            add(MT - 1)
+            return lambda: add(MT - 1)
 
         def content(G):
             for m in range(MT):
@@ -252,6 +252,7 @@ def tile_multiheadlatentattention_pb_kernel(tc, x, cos, sin, wq, out):
         pending = []
         done = set()
         pe_jobs = []
+        late_adds = []
         n = len(steps)
         for t in range(-LS - 1, n + 4):
             if t == 1:
@@ -271,11 +272,14 @@ def tile_multiheadlatentattention_pb_kernel(tc, x, cos, sin, wq, out):
             if 1 <= t <= n:
                 quant(steps[t - 1][0])
                 pe_jobs.extend(steps[t - 1][0])
+            for last_add in late_adds:
+                last_add()
+            late_adds.clear()
             for job in [j for j in pending if j[0] <= t]:
                 pending.remove(job)
                 done.add((job[2], job[1]))
                 if job[1] == ROPE:
-                    rope(job[2])
+                    late_adds.append(rope(job[2]))
                 else:
                     content(job[2])
             if t >= 2:

@@ -20,15 +20,22 @@ GW = 1024
 ROPE, CONTENT = 1, 0
 
 RAWBUFS = 8
-LS = 0
-GRPBUFS = LS + 3
-WCBUFS = 6
+GRPBUFS = 4
+WCBUFS = 8
+OTBUFS = 10
+K4BUFS = 8
 G_ADDS = 3
-MERGE_MUL = True
-IL4 = True
+CHUNKS = 4
 ROPE_LAG = 1
 CONTENT_LAG = 2
-S_HEADS = [1,1,0,2,2,3,1,2,4,2,2,2,3,3,0,3,4,2,2,4,4,2,1,2,4,2,3,3,4,4,3,4]
+MERGE = True
+MOVED_STEPS = 14
+HEAD_SH = [(2, 0), (2, 0), (2, 0), (2, 0)]
+MID_SH = [(3, 0), (3, 0), (3, 0), (3, 0)]
+LAST_SH = [(3, 0), (3, 0), (4, 4), (3, 0), (4, 0)]
+PASS_ORDER = (ROPE, CONTENT)
+LAG_A = 1
+LAG_B = 1
 
 
 def tile_multiheadlatentattention_pb_kernel(tc, x, cos, sin, wq, out):
@@ -39,89 +46,128 @@ def tile_multiheadlatentattention_pb_kernel(tc, x, cos, sin, wq, out):
     with ExitStack() as ctx:
         const = ctx.enter_context(tc.tile_pool(name="const", bufs=1))
         rawp = ctx.enter_context(tc.tile_pool(name="rawp", bufs=RAWBUFS))
-        k4p = ctx.enter_context(tc.tile_pool(name="k4p", bufs=8))
+        k4p = ctx.enter_context(tc.tile_pool(name="k4p", bufs=K4BUFS))
         grpp = ctx.enter_context(tc.tile_pool(name="grpp", bufs=GRPBUFS))
         wcp = ctx.enter_context(tc.tile_pool(name="wcp", bufs=WCBUFS))
-        otp = ctx.enter_context(tc.tile_pool(name="otp", bufs=3))
+        otp = ctx.enter_context(tc.tile_pool(name="otp", bufs=OTBUFS))
         psum = ctx.enter_context(tc.psum_pool(name="psum", bufs=1))
         ctx.enter_context(tc.manual_schedule())
 
         ident = const.tile([P, P], F32, name="ident")
+        identb = const.tile([P, P], BF16, name="identb")
         cos_sb = const.tile([P, 64], BF16, name="cos_sb")
         sin_sb = const.tile([P, 64], BF16, name="sin_sb")
         tab = const.tile([P, 2, 512], F32, name="tab")
         warm = const.tile([P, 8], F32, name="warm")
         warm2 = const.tile([P, 8], F32, name="warm2")
-        xcodes = const.tile([P, MT, 512], U32, name="xcodes", align_bytes=64)
-        xscales = const.tile([P, MT, 512], U8, name="xscales", align_bytes=64)
+        xcodes = const.tile([P, NPASS, 512], U32, name="xcodes", align_bytes=64)
+        xscales = const.tile([P, NPASS, 512], U8, name="xscales", align_bytes=64)
 
-        raw, xs, xg, grp, wcodes, wscales, acc, ot = {}, {}, {}, {}, {}, {}, {}, {}
+        raw, xk, xg, grp, wcodes, wscales, acc, ot, moved = {}, {}, {}, {}, {}, {}, {}, {}, {}
+        parts = {}
 
         def bank(i, shape):
             return psum.tile(shape, F32, name="bank%d" % i)
 
         def load_raw(s):
             G, g = s // NPASS, s % NPASS
-            t = rawp.tile([P, 4, GW], BF16, name="raw")
-            raw[(G, g)] = t
-            nc.sync.dma_start(
-                out=t[:],
-                in_=wq[512 * g : 512 * (g + 1), GW * G : GW * (G + 1)].rearrange("(p j) w -> p j w", j=4),
-            )
+            nch = CHUNKS if s == 0 else 1
+            nh = 4 // nch
+            pieces = []
+            for c in range(nch):
+                t = rawp.tile([P, 4, 256 * nh], BF16, name="raw")
+                pieces.append((t, nh * c, nh))
+                nc.sync.dma_start(
+                    out=t[:],
+                    in_=wq[512 * g : 512 * (g + 1), GW * G + 256 * nh * c : GW * G + 256 * nh * (c + 1)].rearrange("(p j) w -> p j w", j=4),
+                )
+            raw[(G, g)] = pieces
 
-        def load_x(m):
-            t = k4p.tile([P, E], BF16, name="k4", align_bytes=64)
-            xs[m] = t
-            nc.sync.dma_start(out=t[:], in_=x_rows[P * m : P * (m + 1), :])
+        def load_x(g):
+            t = k4p.tile([P, MT, 512], BF16, name="k4", align_bytes=64)
+            xk[g] = t
+            nc.sync.dma_start(out=t[:], in_=x_rows[:, 512 * g : 512 * (g + 1)].rearrange("(m p) k -> p m k", p=P))
 
-        def x_turn(m):
-            words = xs[m][:].bitcast(F32)
+        def x_turn(g):
+            words = xk[g][:].bitcast(F32)
             t = k4p.tile([P, E], BF16, name="k4", align_bytes=64)
-            xg[m] = t
-            xgw = t[:].bitcast(F32).rearrange("p (g r u) -> p g r u", g=NPASS, u=2)
+            xg[g] = t
+            xgw = t[:].bitcast(F32).rearrange("p (m r u) -> p m r u", m=MT, u=2)
             for half in range(2):
-                tp = bank(2 * m + half, [P, 4, P])
-                for gg in range(2):
-                    g = 2 * half + gg
+                tp = bank(half, [P, 4, P])
+                for mm in range(2):
                     for u in range(2):
-                        nc.tensor.transpose(tp[:, 2 * gg + u, :], words[:, 256 * g + u : 256 * (g + 1) : 2], ident[:])
+                        nc.tensor.transpose(tp[:, 2 * mm + u, :], words[:, 2 * half + mm, u : 256 : 2], ident[:])
                 nc.scalar.copy(
                     out=xgw[:, 2 * half : 2 * half + 2],
-                    in_=tp[:].rearrange("p (g u) r -> p g r u", u=2),
+                    in_=tp[:].rearrange("p (m u) r -> p m r u", u=2),
                 )
 
-        def x_quant(m):
-            nc.vector.quantize_mx(out=xcodes[:, m, :].bitcast(E5X4), scales=xscales[:, m, :], in_=xg[m][:])
+        def x_quant(g):
+            nc.vector.quantize_mx(out=xcodes[:, g, :].bitcast(E5X4), scales=xscales[:, g, :], in_=xg[g][:])
 
-        def il_views(u):
+        def il(copy, u, lo, hi, even):
             G, kind, g = u
-            if IL4:
-                dst = grp[u].rearrange("p (h b i j) -> p h b j i", h=4, i=4, j=4)
-                src = raw[(G, g)][:].rearrange("p j (h k b i) -> p k h b j i", k=2, b=32, i=4)[:, kind]
-            else:
-                dst = grp[u].rearrange("p (h c j) -> p h c j", h=4, j=4)
-                src = raw[(G, g)][:].rearrange("p j (h k c) -> p k h c j", k=2, c=128)[:, kind]
-            return dst, src
+            dst = grp[u].rearrange("p (h b i j) -> p h b j i", h=4, i=4, j=4)
+            for t, h0, nh in raw[(G, g)]:
+                a, b = max(lo, h0), min(hi, h0 + nh)
+                if a >= b:
+                    continue
+                src = t[:].rearrange("p j (h k b i) -> p k h b j i", k=2, b=32, i=4)[:, kind]
+                cuts = [(a, b)]
+                if even and b - a == 3:
+                    cuts = [(a, a + 2), (a + 2, b)]
+                for c0, c1 in cuts:
+                    copy(out=dst[:, c0:c1], in_=src[:, c0 - h0 : c1 - h0])
 
-        def il_scalar(units, heads):
+        def move(a):
+            G, kind, g = steps[a][0][1]
+            tiles = []
+            for h in range(1, 4):
+                if h % 2 == 1:
+                    tiles.append(psum.tile([P, 1024], BF16, name="bank%d" % (2 + h // 2)))
+                for t, h0, nh in raw[(G, g)]:
+                    if h0 <= h < h0 + nh:
+                        nc.tensor.matmul(
+                            out=tiles[-1][:, 512 * ((h - 1) % 2) : 512 * ((h - 1) % 2 + 1)].rearrange("p (c j) -> p c j", j=4),
+                            lhsT=identb[:],
+                            rhs=t[:].rearrange("p j (h k c) -> p k h c j", k=2, c=128)[:, kind, h - h0],
+                            start=True,
+                            stop=True,
+                        )
+            moved[a] = tiles
+
+        def v_heads(a, i):
+            if i == 1 and a < MOVED_STEPS:
+                return 1
+            return 4 - steps[a][1][i]
+
+        def il_scalar(a):
+            units = steps[a][0]
             t = grpp.tile([P, 2, 2048], BF16, name="grp", align_bytes=64)
             for i in range(len(units)):
                 grp[units[i]] = t[:, i, :]
             grp[tuple(units)] = t
             for i in range(len(units)):
-                dst, src = il_views(units[i])
-                if heads[i] > 0:
-                    nc.scalar.copy(out=dst[:, 0 : heads[i]], in_=src[:, 0 : heads[i]])
+                if not (i == 1 and a < MOVED_STEPS):
+                    il(nc.scalar.copy, units[i], v_heads(a, i), 4, False)
+            if a < MOVED_STEPS:
+                nc.scalar.copy(out=t[:, 1, 512:1536], in_=moved[a][0][:])
+                nc.scalar.copy(out=t[:, 1, 1536:2048], in_=moved[a][1][:, 0:512])
 
-        def il_vector(units, heads):
+        def il_vector(a):
+            units = steps[a][0]
+            both = 0
+            if MERGE and len(units) == 2 and units[0][0] == units[1][0] and units[0][2] == units[1][2]:
+                both = min(v_heads(a, 0), v_heads(a, 1))
+                G, kind, g = units[0]
+                dst = grp[tuple(units)][:].rearrange("p i (h b q j) -> p h i b j q", h=4, q=4, j=4)
+                for t, h0, nh in raw[(G, g)]:
+                    src = t[:].rearrange("p j (h k b q) -> p h k b j q", k=2, b=32, q=4)
+                    for h in range(max(0, h0), min(both, h0 + nh)):
+                        nc.vector.tensor_copy(out=dst[:, h], in_=src[:, h - h0])
             for i in range(len(units)):
-                dst, src = il_views(units[i])
-                lo = heads[i]
-                if lo == 1:
-                    nc.vector.tensor_copy(out=dst[:, 1:3], in_=src[:, 1:3])
-                    nc.vector.tensor_copy(out=dst[:, 3:4], in_=src[:, 3:4])
-                elif lo < 4:
-                    nc.vector.tensor_copy(out=dst[:, lo:4], in_=src[:, lo:4])
+                il(nc.vector.tensor_copy, units[i], both, v_heads(a, i), True)
 
         def quant(units):
             n = len(units)
@@ -136,43 +182,38 @@ def tile_multiheadlatentattention_pb_kernel(tc, x, cos, sin, wq, out):
                 in_=t[:, 0:n, :].rearrange("p a w -> p (a w)"),
             )
 
-        def passes(u):
+        def one_pass(u, m):
             G, kind, g = u
-            for m in range(MT):
-                if g == 0:
-                    a = bank(4 * kind + m, [P, 512])
-                    acc[(G, kind, m)] = a
-                nc.tensor.matmul_mx(
-                    out=acc[(G, kind, m)][:],
-                    lhsT=xcodes[:, m, P * g : P * (g + 1)].bitcast(E5X4),
-                    lhsT_scale=xscales[:, m, P * g : P * (g + 1)],
-                    rhs=wcodes[u].bitcast(E5X4),
-                    rhs_scale=wscales[u],
-                    start=(g == 0),
-                    stop=(g == NPASS - 1),
-                )
+            if g == 0:
+                acc[(G, kind, m)] = bank(4 * kind + (m if (kind == ROPE or G == GROUPS - 1) else m % 2), [P, 512])
+            nc.tensor.matmul_mx(
+                out=acc[(G, kind, m)][:],
+                lhsT=xcodes[:, g, P * m : P * (m + 1)].bitcast(E5X4),
+                lhsT_scale=xscales[:, g, P * m : P * (m + 1)],
+                rhs=wcodes[u].bitcast(E5X4),
+                rhs_scale=wscales[u],
+                start=(g == 0),
+                stop=(g == NPASS - 1),
+            )
 
-        def ot_part(G, kind):
-            if G == GROUPS - 1:
-                return ot[G][:, kind].rearrange("p m (h c) -> p m h c", c=128)
-            return ot[G][:].rearrange("p m (h k c) -> p k m h c", k=2, c=128)[:, kind]
+        def ot_tile(G, m):
+            if (G, m) not in ot:
+                ot[(G, m)] = otp.tile([P, GW], F32, name="ot")
+            return ot[(G, m)]
+
+        def ot_part(G, m, kind):
+            return ot_tile(G, m)[:].rearrange("p (h k c) -> p k h c", k=2, c=128)[:, kind]
 
         def store(G, m, kind):
             rows = out_rows[P * m : P * (m + 1), GW * G : GW * (G + 1)]
             if G == GROUPS - 1:
-                nc.sync.dma_start(
-                    out=rows.rearrange("p (h k c) -> p k h c", k=2, c=128)[:, kind],
-                    in_=ot[G][:, kind, m, :].rearrange("p (h c) -> p h c", c=128),
-                )
-            elif kind == CONTENT:
-                nc.sync.dma_start(out=rows, in_=ot[G][:, m, :])
+                nc.sync.dma_start(out=rows.rearrange("p (h k c) -> p k h c", k=2, c=128)[:, kind], in_=ot_part(G, m, kind))
+            else:
+                parts[(G, m)] = parts.get((G, m), 0) + 1
+                if parts[(G, m)] == 2:
+                    nc.sync.dma_start(out=rows, in_=ot_tile(G, m)[:])
 
         def rope(G):
-            if G == GROUPS - 1:
-                o = otp.tile([P, 2, MT, 512], F32, name="ot")
-            else:
-                o = otp.tile([P, MT, GW], F32, name="ot")
-            ot[G] = o
             prod = {}
 
             def mul(m):
@@ -189,7 +230,7 @@ def tile_multiheadlatentattention_pb_kernel(tc, x, cos, sin, wq, out):
             def add(m):
                 eng = nc.gpsimd if m < G_ADDS else nc.vector
                 eng.tensor_tensor(
-                    out=ot_part(G, ROPE)[:, m],
+                    out=ot_part(G, m, ROPE),
                     in0=prod[m][:, 0, :].rearrange("p (h c) -> p h c", c=128),
                     in1=prod[m][:, 1, :].rearrange("p (h c) -> p h c", c=128),
                     op=ALU.add,
@@ -202,101 +243,144 @@ def tile_multiheadlatentattention_pb_kernel(tc, x, cos, sin, wq, out):
                 add(m - 1)
             return lambda: add(MT - 1)
 
-        def content(G):
-            for m in range(MT):
+        def content(G, ms):
+            for m in ms:
                 src = acc[(G, CONTENT, m)][:].rearrange("p (h c) -> p h c", c=128)
                 if G == GROUPS - 1 and m % 2 == 1:
-                    nc.vector.tensor_copy(out=ot_part(G, CONTENT)[:, m], in_=src)
+                    nc.vector.tensor_copy(out=ot_part(G, m, CONTENT), in_=src)
                 else:
-                    nc.scalar.copy(out=ot_part(G, CONTENT)[:, m], in_=src)
+                    nc.scalar.copy(out=ot_part(G, m, CONTENT), in_=src)
                 store(G, m, CONTENT)
 
-        nc.scalar.dma_start(out=cos_sb[:], in_=cos)
-        nc.scalar.dma_start(out=sin_sb[:], in_=sin)
+
         nc.vector.memset(warm[:], 0.0)
         nc.scalar.copy(out=warm2[:], in_=warm[:])
         make_identity(nc, ident[:])
-        load_raw(0)
-        load_x(0)
-        load_x(1)
-        load_raw(1)
-        load_x(2)
-        load_x(3)
-        for s in range(2, RAWBUFS):
+        make_identity(nc, identb[:])
+        slots = RAWBUFS
+        nxt = 0
+        for s in range(NPASS):
             load_raw(s)
-        next_raw = [RAWBUFS]
+            if s == 0:
+                nc.sync.dma_start(out=cos_sb[:], in_=cos)
+                nc.sync.dma_start(out=sin_sb[:], in_=sin)
+            load_x(s)
+            slots -= CHUNKS if s == 0 else 1
+            nxt += 1
+        while slots > 0:
+            load_raw(nxt)
+            nxt += 1
+            slots -= 1
+        next_raw = [nxt]
 
-        tv = tab[:].rearrange("p t (h j e) -> p t h j e", h=4, e=2)
-        for h in range(4):
-            for e in range(2):
-                nc.vector.tensor_copy(out=tv[:, e, h, :, e], in_=cos_sb[:])
-                nc.vector.tensor_scalar_mul(out=tv[:, e, h, :, 1 - e], in0=sin_sb[:], scalar1=(1.0 if e == 0 else -1.0))
+        def build_tables():
+            tv = tab[:].rearrange("p t (h j e) -> p t h j e", h=4, e=2)
+            for h in range(4):
+                for e in range(2):
+                    nc.vector.tensor_copy(out=tv[:, e, h, :, e], in_=cos_sb[:])
+                    nc.vector.tensor_scalar_mul(out=tv[:, e, h, :, 1 - e], in0=sin_sb[:], scalar1=(1.0 if e == 0 else -1.0))
 
-        prep = []
-        for G in range(GROUPS):
-            if G < GROUPS - 1:
-                for g in range(NPASS):
-                    prep.append((G, ROPE, g))
-                    prep.append((G, CONTENT, g))
-            else:
-                for kind in (ROPE, CONTENT):
-                    for g in range(NPASS):
-                        prep.append((G, kind, g))
         steps = []
-        for i in range(0, len(prep) - 2, 2):
-            steps.append(([prep[i], prep[i + 1]], [S_HEADS[i], S_HEADS[i + 1]]))
-        steps.append(([prep[-2]], [S_HEADS[-2]]))
-        steps.append(([prep[-1]], [S_HEADS[-1]]))
+        for G in range(GROUPS - 1):
+            for g in range(NPASS):
+                s = NPASS * G + g
+                sh = HEAD_SH[s] if s < len(HEAD_SH) else MID_SH[s % len(MID_SH)]
+                steps.append(([(G, CONTENT, g), (G, ROPE, g)], [sh[0], sh[1]]))
+        G = GROUPS - 1
+        last = [(G, ROPE, g) for g in range(NPASS)] + [(G, CONTENT, g) for g in range(NPASS)]
+        for i in range(3):
+            steps.append(([last[2 * i], last[2 * i + 1]], [LAST_SH[i][0], LAST_SH[i][1]]))
+        steps.append(([last[6]], [LAST_SH[3][0]]))
+        steps.append(([last[7]], [LAST_SH[4][0]]))
 
         uses = {}
         pending = []
         done = set()
-        pe_jobs = []
+        queues = {ROPE: [], CONTENT: []}
         late_adds = []
         n = len(steps)
-        for t in range(-LS - 1, n + 4):
-            if t == 1:
-                x_quant(0)
-                x_quant(1)
-            if t == 2:
-                x_quant(2)
-                x_quant(3)
+
+        def free_raw(units):
+            for u in units:
+                key = (u[0], u[2])
+                uses[key] = uses.get(key, 0) + 1
+                if uses[key] == 2:
+                    for i in range(len(raw[key])):
+                        if next_raw[0] < GROUPS * NPASS:
+                            load_raw(next_raw[0])
+                            next_raw[0] += 1
+
+        def write_passes(t):
+            for kind in PASS_ORDER:
+                q = queues[kind]
+                while len(q) > 0:
+                    u = q[0]
+                    if u[2] == 0 and u[0] > 0 and (u[0] - 1, kind) not in done:
+                        break
+                    if kind == CONTENT and u[0] == 0 and t < NPASS - 1:
+                        break
+                    if u[0] == 0 and u[2] not in xq_done:
+                        break
+                    split = kind == CONTENT and u[0] < GROUPS - 1
+                    for m in range(2 if split else MT):
+                        one_pass(u, m)
+                    q.pop(0)
+                    if u[2] == NPASS - 1:
+                        if kind == ROPE:
+                            pending.append((t + ROPE_LAG, "rope", u[0]))
+                        elif split:
+                            pending.append((t + LAG_A, "first", u[0]))
+                        else:
+                            pending.append((t + CONTENT_LAG, "all", u[0]))
+
+        xq_done = set()
+
+        def do_quant(s):
+            quant(steps[s][0])
+            for u in steps[s][0]:
+                queues[u[1]].append(u)
+
+        move(0)
+        for t in range(-1, n + 7):
+            a = t + 1
+            for job in [j for j in pending if j[0] <= t and j[1] != "rope"]:
+                pending.remove(job)
+                G = job[2]
+                if job[1] == "first":
+                    content(G, [0, 1])
+                    for m in (2, 3):
+                        for g in range(NPASS):
+                            one_pass((G, CONTENT, g), m)
+                    pending.append((t + LAG_B, "second", G))
+                elif job[1] == "second":
+                    content(G, [2, 3])
+                    done.add((G, CONTENT))
+                else:
+                    content(G, [0, 1, 2, 3])
+                    done.add((G, CONTENT))
+            if 0 <= a < n:
+                il_scalar(a)
+            if 0 <= a < NPASS:
+                x_turn(a)
             if 0 <= t < n:
-                il_vector(steps[t][0], steps[t][1])
-                for u in steps[t][0]:
-                    key = (u[0], u[2])
-                    uses[key] = uses.get(key, 0) + 1
-                    if uses[key] == 2 and next_raw[0] < GROUPS * NPASS:
-                        load_raw(next_raw[0])
-                        next_raw[0] += 1
-            if 1 <= t <= n:
-                quant(steps[t - 1][0])
-                pe_jobs.extend(steps[t - 1][0])
+                il_vector(t)
+                free_raw(steps[t][0])
+            if t == 0:
+                build_tables()
+            if 1 <= t <= NPASS:
+                x_quant(t - 1)
+                xq_done.add(t - 1)
+            if 0 <= t < NPASS:
+                do_quant(t)
+            if NPASS < t <= n:
+                do_quant(t - 1)
             for last_add in late_adds:
                 last_add()
             late_adds.clear()
-            for job in [j for j in pending if j[0] <= t]:
+            for job in [j for j in pending if j[0] <= t and j[1] == "rope"]:
                 pending.remove(job)
-                done.add((job[2], job[1]))
-                if job[1] == ROPE:
-                    late_adds.append(rope(job[2]))
-                else:
-                    content(job[2])
-            if t >= 2:
-                while len(pe_jobs) > 0:
-                    u = pe_jobs[0]
-                    if u[2] == 0 and u[0] > 0 and (u[0] - 1, u[1]) not in done:
-                        break
-                    passes(u)
-                    pe_jobs.pop(0)
-                    if u[2] == NPASS - 1:
-                        pending.append((t + (ROPE_LAG if u[1] == ROPE else CONTENT_LAG), u[1], u[0]))
-            a = t + LS + 1
-            if 0 <= a < n:
-                il_scalar(steps[a][0], steps[a][1])
-            if a == 0:
-                x_turn(0)
-                x_turn(1)
-            if a == 1:
-                x_turn(2)
-                x_turn(3)
+                done.add((job[2], ROPE))
+                late_adds.append(rope(job[2]))
+            write_passes(t)
+            if 0 <= a + 1 < MOVED_STEPS:
+                move(a + 1)

@@ -20,22 +20,18 @@ GW = 1024
 ROPE, CONTENT = 1, 0
 
 RAWBUFS = 8
-GRPBUFS = 4
-WCBUFS = 8
+GRPBUFS = 3
+WCBUFS = 6
 OTBUFS = 10
 K4BUFS = 8
 G_ADDS = 3
 CHUNKS = 4
 ROPE_LAG = 1
 CONTENT_LAG = 2
-MERGE = True
-MOVED_STEPS = 14
-HEAD_SH = [(2, 0), (2, 0), (2, 0), (2, 0)]
-MID_SH = [(3, 0), (3, 0), (3, 0), (3, 0)]
-LAST_SH = [(3, 0), (3, 0), (4, 4), (3, 0), (4, 0)]
-PASS_ORDER = (ROPE, CONTENT)
-LAG_A = 1
-LAG_B = 1
+HEAD_COLS = 64
+MID_COLS = 76
+LAST_COLS = [96, 96, 128, 96, 128]
+Q_FIRST = 4
 
 
 def tile_multiheadlatentattention_pb_kernel(tc, x, cos, sin, wq, out):
@@ -54,17 +50,15 @@ def tile_multiheadlatentattention_pb_kernel(tc, x, cos, sin, wq, out):
         ctx.enter_context(tc.manual_schedule())
 
         ident = const.tile([P, P], F32, name="ident")
-        identb = const.tile([P, P], BF16, name="identb")
         cos_sb = const.tile([P, 64], BF16, name="cos_sb")
         sin_sb = const.tile([P, 64], BF16, name="sin_sb")
-        tab = const.tile([P, 2, 512], F32, name="tab")
+        tab = const.tile([P, 2, 128], F32, name="tab")
         warm = const.tile([P, 8], F32, name="warm")
         warm2 = const.tile([P, 8], F32, name="warm2")
         xcodes = const.tile([P, NPASS, 512], U32, name="xcodes", align_bytes=64)
         xscales = const.tile([P, NPASS, 512], U8, name="xscales", align_bytes=64)
 
-        raw, xk, xg, grp, wcodes, wscales, acc, ot, moved = {}, {}, {}, {}, {}, {}, {}, {}, {}
-        parts = {}
+        raw, xk, xg, grp, wcodes, wscales, acc, ot = {}, {}, {}, {}, {}, {}, {}, {}
 
         def bank(i, shape):
             return psum.tile(shape, F32, name="bank%d" % i)
@@ -94,7 +88,7 @@ def tile_multiheadlatentattention_pb_kernel(tc, x, cos, sin, wq, out):
             xg[g] = t
             xgw = t[:].bitcast(F32).rearrange("p (m r u) -> p m r u", m=MT, u=2)
             for half in range(2):
-                tp = bank(half, [P, 4, P])
+                tp = bank(2 * (g % 2) + half, [P, 4, P])
                 for mm in range(2):
                     for u in range(2):
                         nc.tensor.transpose(tp[:, 2 * mm + u, :], words[:, 2 * half + mm, u : 256 : 2], ident[:])
@@ -106,68 +100,32 @@ def tile_multiheadlatentattention_pb_kernel(tc, x, cos, sin, wq, out):
         def x_quant(g):
             nc.vector.quantize_mx(out=xcodes[:, g, :].bitcast(E5X4), scales=xscales[:, g, :], in_=xg[g][:])
 
-        def il(copy, u, lo, hi, even):
-            G, kind, g = u
-            dst = grp[u].rearrange("p (h b i j) -> p h b j i", h=4, i=4, j=4)
-            for t, h0, nh in raw[(G, g)]:
-                a, b = max(lo, h0), min(hi, h0 + nh)
-                if a >= b:
-                    continue
-                src = t[:].rearrange("p j (h k b i) -> p k h b j i", k=2, b=32, i=4)[:, kind]
-                cuts = [(a, b)]
-                if even and b - a == 3:
-                    cuts = [(a, a + 2), (a + 2, b)]
-                for c0, c1 in cuts:
-                    copy(out=dst[:, c0:c1], in_=src[:, c0 - h0 : c1 - h0])
-
-        def move(a):
-            G, kind, g = steps[a][0][1]
-            tiles = []
-            for h in range(1, 4):
-                if h % 2 == 1:
-                    tiles.append(psum.tile([P, 1024], BF16, name="bank%d" % (2 + h // 2)))
+        def il(copy, units, lo, hi):
+            if lo >= hi:
+                return
+            if len(units) == 2 and units[0][0] == units[1][0] and units[0][2] == units[1][2]:
+                G, kind, g = units[0]
+                dst = grp[tuple(units)][:].rearrange("p k (h c j) -> p h k c j", h=4, j=4)
                 for t, h0, nh in raw[(G, g)]:
-                    if h0 <= h < h0 + nh:
-                        nc.tensor.matmul(
-                            out=tiles[-1][:, 512 * ((h - 1) % 2) : 512 * ((h - 1) % 2 + 1)].rearrange("p (c j) -> p c j", j=4),
-                            lhsT=identb[:],
-                            rhs=t[:].rearrange("p j (h k c) -> p k h c j", k=2, c=128)[:, kind, h - h0],
-                            start=True,
-                            stop=True,
-                        )
-            moved[a] = tiles
+                    src = t[:].rearrange("p j (h k c) -> p h k c j", k=2, c=128)
+                    copy(out=dst[:, h0 : h0 + nh, :, lo:hi], in_=src[:, :, :, lo:hi])
+            else:
+                for u in units:
+                    G, kind, g = u
+                    dst = grp[u].rearrange("p (h c j) -> p h c j", h=4, j=4)
+                    for t, h0, nh in raw[(G, g)]:
+                        src = t[:].rearrange("p j (h k c) -> p k h c j", k=2, c=128)[:, kind]
+                        copy(out=dst[:, h0 : h0 + nh, lo:hi], in_=src[:, :, lo:hi])
 
-        def v_heads(a, i):
-            if i == 1 and a < MOVED_STEPS:
-                return 1
-            return 4 - steps[a][1][i]
-
-        def il_scalar(a):
-            units = steps[a][0]
+        def il_scalar(units, cols):
             t = grpp.tile([P, 2, 2048], BF16, name="grp", align_bytes=64)
             for i in range(len(units)):
                 grp[units[i]] = t[:, i, :]
             grp[tuple(units)] = t
-            for i in range(len(units)):
-                if not (i == 1 and a < MOVED_STEPS):
-                    il(nc.scalar.copy, units[i], v_heads(a, i), 4, False)
-            if a < MOVED_STEPS:
-                nc.scalar.copy(out=t[:, 1, 512:1536], in_=moved[a][0][:])
-                nc.scalar.copy(out=t[:, 1, 1536:2048], in_=moved[a][1][:, 0:512])
+            il(nc.scalar.copy, units, 128 - cols, 128)
 
-        def il_vector(a):
-            units = steps[a][0]
-            both = 0
-            if MERGE and len(units) == 2 and units[0][0] == units[1][0] and units[0][2] == units[1][2]:
-                both = min(v_heads(a, 0), v_heads(a, 1))
-                G, kind, g = units[0]
-                dst = grp[tuple(units)][:].rearrange("p i (h b q j) -> p h i b j q", h=4, q=4, j=4)
-                for t, h0, nh in raw[(G, g)]:
-                    src = t[:].rearrange("p j (h k b q) -> p h k b j q", k=2, b=32, q=4)
-                    for h in range(max(0, h0), min(both, h0 + nh)):
-                        nc.vector.tensor_copy(out=dst[:, h], in_=src[:, h - h0])
-            for i in range(len(units)):
-                il(nc.vector.tensor_copy, units[i], both, v_heads(a, i), True)
+        def il_vector(units, cols):
+            il(nc.vector.tensor_copy, units, 0, 128 - cols)
 
         def quant(units):
             n = len(units)
@@ -185,7 +143,7 @@ def tile_multiheadlatentattention_pb_kernel(tc, x, cos, sin, wq, out):
         def one_pass(u, m):
             G, kind, g = u
             if g == 0:
-                acc[(G, kind, m)] = bank(4 * kind + (m if (kind == ROPE or G == GROUPS - 1) else m % 2), [P, 512])
+                acc[(G, kind, m)] = bank(4 * kind + m, [P, 512])
             nc.tensor.matmul_mx(
                 out=acc[(G, kind, m)][:],
                 lhsT=xcodes[:, g, P * m : P * (m + 1)].bitcast(E5X4),
@@ -208,10 +166,8 @@ def tile_multiheadlatentattention_pb_kernel(tc, x, cos, sin, wq, out):
             rows = out_rows[P * m : P * (m + 1), GW * G : GW * (G + 1)]
             if G == GROUPS - 1:
                 nc.sync.dma_start(out=rows.rearrange("p (h k c) -> p k h c", k=2, c=128)[:, kind], in_=ot_part(G, m, kind))
-            else:
-                parts[(G, m)] = parts.get((G, m), 0) + 1
-                if parts[(G, m)] == 2:
-                    nc.sync.dma_start(out=rows, in_=ot_tile(G, m)[:])
+            elif kind == SECOND[G]:
+                nc.sync.dma_start(out=rows, in_=ot_tile(G, m)[:])
 
         def rope(G):
             prod = {}
@@ -221,9 +177,9 @@ def tile_multiheadlatentattention_pb_kernel(tc, x, cos, sin, wq, out):
                 t = k4p.tile([P, 2, 512], F32, name="k4", align_bytes=64)
                 prod[m] = t
                 nc.vector.tensor_tensor(
-                    out=t[:].rearrange("p o (q e) -> p o q e", e=2),
-                    in0=tab[:].rearrange("p o (q e) -> p o q e", e=2),
-                    in1=a[:].rearrange("p (q o z) -> p o q z", o=2, z=1).to_broadcast([P, 2, 256, 2]),
+                    out=t[:].rearrange("p o (h q e) -> p o h q e", h=4, e=2),
+                    in0=tab[:].rearrange("p o (z q e) -> p o z q e", z=1, e=2).to_broadcast([P, 2, 4, 64, 2]),
+                    in1=a[:].rearrange("p (h q o z) -> p o h q z", h=4, o=2, z=1).to_broadcast([P, 2, 4, 64, 2]),
                     op=ALU.mult,
                 )
 
@@ -243,8 +199,8 @@ def tile_multiheadlatentattention_pb_kernel(tc, x, cos, sin, wq, out):
                 add(m - 1)
             return lambda: add(MT - 1)
 
-        def content(G, ms):
-            for m in ms:
+        def content(G):
+            for m in range(MT):
                 src = acc[(G, CONTENT, m)][:].rearrange("p (h c) -> p h c", c=128)
                 if G == GROUPS - 1 and m % 2 == 1:
                     nc.vector.tensor_copy(out=ot_part(G, m, CONTENT), in_=src)
@@ -252,18 +208,17 @@ def tile_multiheadlatentattention_pb_kernel(tc, x, cos, sin, wq, out):
                     nc.scalar.copy(out=ot_part(G, m, CONTENT), in_=src)
                 store(G, m, CONTENT)
 
+        SECOND = [CONTENT, CONTENT, CONTENT, CONTENT]
 
         nc.vector.memset(warm[:], 0.0)
         nc.scalar.copy(out=warm2[:], in_=warm[:])
         make_identity(nc, ident[:])
-        make_identity(nc, identb[:])
         slots = RAWBUFS
         nxt = 0
+        nc.sync.dma_start(out=cos_sb[:], in_=cos)
+        nc.sync.dma_start(out=sin_sb[:], in_=sin)
         for s in range(NPASS):
             load_raw(s)
-            if s == 0:
-                nc.sync.dma_start(out=cos_sb[:], in_=cos)
-                nc.sync.dma_start(out=sin_sb[:], in_=sin)
             load_x(s)
             slots -= CHUNKS if s == 0 else 1
             nxt += 1
@@ -274,24 +229,23 @@ def tile_multiheadlatentattention_pb_kernel(tc, x, cos, sin, wq, out):
         next_raw = [nxt]
 
         def build_tables():
-            tv = tab[:].rearrange("p t (h j e) -> p t h j e", h=4, e=2)
-            for h in range(4):
-                for e in range(2):
-                    nc.vector.tensor_copy(out=tv[:, e, h, :, e], in_=cos_sb[:])
-                    nc.vector.tensor_scalar_mul(out=tv[:, e, h, :, 1 - e], in0=sin_sb[:], scalar1=(1.0 if e == 0 else -1.0))
+            tv = tab[:].rearrange("p t (j e) -> p t j e", e=2)
+            for e in range(2):
+                nc.scalar.copy(out=tv[:, e, :, e], in_=cos_sb[:])
+                nc.scalar.mul(out=tv[:, e, :, 1 - e], in_=sin_sb[:], mul=(1.0 if e == 0 else -1.0))
 
+        build_tables()
         steps = []
         for G in range(GROUPS - 1):
             for g in range(NPASS):
                 s = NPASS * G + g
-                sh = HEAD_SH[s] if s < len(HEAD_SH) else MID_SH[s % len(MID_SH)]
-                steps.append(([(G, CONTENT, g), (G, ROPE, g)], [sh[0], sh[1]]))
+                steps.append(([(G, CONTENT, g), (G, ROPE, g)], HEAD_COLS if s < NPASS else MID_COLS))
         G = GROUPS - 1
         last = [(G, ROPE, g) for g in range(NPASS)] + [(G, CONTENT, g) for g in range(NPASS)]
         for i in range(3):
-            steps.append(([last[2 * i], last[2 * i + 1]], [LAST_SH[i][0], LAST_SH[i][1]]))
-        steps.append(([last[6]], [LAST_SH[3][0]]))
-        steps.append(([last[7]], [LAST_SH[4][0]]))
+            steps.append(([last[2 * i], last[2 * i + 1]], LAST_COLS[i]))
+        steps.append(([last[6]], LAST_COLS[3]))
+        steps.append(([last[7]], LAST_COLS[4]))
 
         uses = {}
         pending = []
@@ -311,27 +265,28 @@ def tile_multiheadlatentattention_pb_kernel(tc, x, cos, sin, wq, out):
                             next_raw[0] += 1
 
         def write_passes(t):
-            for kind in PASS_ORDER:
+            for kind in (ROPE, CONTENT):
                 q = queues[kind]
+                if kind == CONTENT and len(q) > 0 and q[0][0] == 0:
+                    if len(q) < NPASS or q[NPASS - 1][0] != 0 or len(xq_done) < NPASS:
+                        continue
+                    for m in range(MT):
+                        for g in range(NPASS):
+                            one_pass(q[g], m)
+                    for g in range(NPASS):
+                        q.pop(0)
+                    pending.append((t + CONTENT_LAG, CONTENT, 0))
                 while len(q) > 0:
                     u = q[0]
                     if u[2] == 0 and u[0] > 0 and (u[0] - 1, kind) not in done:
                         break
-                    if kind == CONTENT and u[0] == 0 and t < NPASS - 1:
-                        break
                     if u[0] == 0 and u[2] not in xq_done:
                         break
-                    split = kind == CONTENT and u[0] < GROUPS - 1
-                    for m in range(2 if split else MT):
+                    for m in range(MT):
                         one_pass(u, m)
                     q.pop(0)
                     if u[2] == NPASS - 1:
-                        if kind == ROPE:
-                            pending.append((t + ROPE_LAG, "rope", u[0]))
-                        elif split:
-                            pending.append((t + LAG_A, "first", u[0]))
-                        else:
-                            pending.append((t + CONTENT_LAG, "all", u[0]))
+                        pending.append((t + (ROPE_LAG if kind == ROPE else CONTENT_LAG), kind, u[0]))
 
         xq_done = set()
 
@@ -340,33 +295,10 @@ def tile_multiheadlatentattention_pb_kernel(tc, x, cos, sin, wq, out):
             for u in steps[s][0]:
                 queues[u[1]].append(u)
 
-        move(0)
-        for t in range(-1, n + 7):
-            a = t + 1
-            for job in [j for j in pending if j[0] <= t and j[1] != "rope"]:
-                pending.remove(job)
-                G = job[2]
-                if job[1] == "first":
-                    content(G, [0, 1])
-                    for m in (2, 3):
-                        for g in range(NPASS):
-                            one_pass((G, CONTENT, g), m)
-                    pending.append((t + LAG_B, "second", G))
-                elif job[1] == "second":
-                    content(G, [2, 3])
-                    done.add((G, CONTENT))
-                else:
-                    content(G, [0, 1, 2, 3])
-                    done.add((G, CONTENT))
-            if 0 <= a < n:
-                il_scalar(a)
-            if 0 <= a < NPASS:
-                x_turn(a)
+        for t in range(-1, n + 5):
             if 0 <= t < n:
-                il_vector(t)
+                il_vector(steps[t][0], steps[t][1])
                 free_raw(steps[t][0])
-            if t == 0:
-                build_tables()
             if 1 <= t <= NPASS:
                 x_quant(t - 1)
                 xq_done.add(t - 1)
@@ -377,10 +309,16 @@ def tile_multiheadlatentattention_pb_kernel(tc, x, cos, sin, wq, out):
             for last_add in late_adds:
                 last_add()
             late_adds.clear()
-            for job in [j for j in pending if j[0] <= t and j[1] == "rope"]:
+            for job in [j for j in pending if j[0] <= t]:
                 pending.remove(job)
-                done.add((job[2], ROPE))
-                late_adds.append(rope(job[2]))
+                done.add((job[2], job[1]))
+                if job[1] == ROPE:
+                    late_adds.append(rope(job[2]))
+                else:
+                    content(job[2])
             write_passes(t)
-            if 0 <= a + 1 < MOVED_STEPS:
-                move(a + 1)
+            a = t + 1
+            if 0 <= a < n:
+                il_scalar(steps[a][0], steps[a][1])
+            if 0 <= a < NPASS:
+                x_turn(a)

@@ -28,9 +28,9 @@ G_ADDS = 3
 CHUNKS = 4
 ROPE_LAG = 1
 CONTENT_LAG = 2
-HEAD_COLS = 64
-MID_COLS = 76
-LAST_COLS = [96, 96, 128, 96, 128]
+HEAD_VB = 32
+MID_VB = 26
+LAST_VB = [16, 16, 0, 8, 0]
 Q_FIRST = 4
 
 
@@ -100,32 +100,26 @@ def tile_multiheadlatentattention_pb_kernel(tc, x, cos, sin, wq, out):
         def x_quant(g):
             nc.vector.quantize_mx(out=xcodes[:, g, :].bitcast(E5X4), scales=xscales[:, g, :], in_=xg[g][:])
 
-        def il(copy, units, lo, hi):
+        def il(copy, u, lo, hi):
             if lo >= hi:
                 return
-            if len(units) == 2 and units[0][0] == units[1][0] and units[0][2] == units[1][2]:
-                G, kind, g = units[0]
-                dst = grp[tuple(units)][:].rearrange("p k (h c j) -> p h k c j", h=4, j=4)
-                for t, h0, nh in raw[(G, g)]:
-                    src = t[:].rearrange("p j (h k c) -> p h k c j", k=2, c=128)
-                    copy(out=dst[:, h0 : h0 + nh, :, lo:hi], in_=src[:, :, :, lo:hi])
-            else:
-                for u in units:
-                    G, kind, g = u
-                    dst = grp[u].rearrange("p (h c j) -> p h c j", h=4, j=4)
-                    for t, h0, nh in raw[(G, g)]:
-                        src = t[:].rearrange("p j (h k c) -> p k h c j", k=2, c=128)[:, kind]
-                        copy(out=dst[:, h0 : h0 + nh, lo:hi], in_=src[:, :, lo:hi])
+            G, kind, g = u
+            dst = grp[u].rearrange("p (h b i j) -> p h b j i", h=4, i=4, j=4)
+            for t, h0, nh in raw[(G, g)]:
+                src = t[:].rearrange("p j (h k b i) -> p k h b j i", k=2, b=32, i=4)[:, kind]
+                copy(out=dst[:, h0 : h0 + nh, lo:hi], in_=src[:, :, lo:hi])
 
-        def il_scalar(units, cols):
+        def il_scalar(units, vb):
             t = grpp.tile([P, 2, 2048], BF16, name="grp", align_bytes=64)
             for i in range(len(units)):
                 grp[units[i]] = t[:, i, :]
             grp[tuple(units)] = t
-            il(nc.scalar.copy, units, 128 - cols, 128)
+            for u in units[:-1]:
+                il(nc.scalar.copy, u, 0, 32)
+            il(nc.scalar.copy, units[-1], vb, 32)
 
-        def il_vector(units, cols):
-            il(nc.vector.tensor_copy, units, 0, 128 - cols)
+        def il_vector(units, vb):
+            il(nc.vector.tensor_copy, units[-1], 0, vb)
 
         def quant(units):
             n = len(units)
@@ -239,13 +233,13 @@ def tile_multiheadlatentattention_pb_kernel(tc, x, cos, sin, wq, out):
         for G in range(GROUPS - 1):
             for g in range(NPASS):
                 s = NPASS * G + g
-                steps.append(([(G, CONTENT, g), (G, ROPE, g)], HEAD_COLS if s < NPASS else MID_COLS))
+                steps.append(([(G, CONTENT, g), (G, ROPE, g)], HEAD_VB if s < NPASS else MID_VB))
         G = GROUPS - 1
         last = [(G, ROPE, g) for g in range(NPASS)] + [(G, CONTENT, g) for g in range(NPASS)]
         for i in range(3):
-            steps.append(([last[2 * i], last[2 * i + 1]], LAST_COLS[i]))
-        steps.append(([last[6]], LAST_COLS[3]))
-        steps.append(([last[7]], LAST_COLS[4]))
+            steps.append(([last[2 * i], last[2 * i + 1]], LAST_VB[i]))
+        steps.append(([last[6]], LAST_VB[3]))
+        steps.append(([last[7]], LAST_VB[4]))
 
         uses = {}
         pending = []

@@ -26,11 +26,12 @@ OTBUFS = 10
 K4BUFS = 8
 G_ADDS = 3
 CHUNKS = 4
+KEEP_WARM = 8
 ROPE_LAG = 1
 CONTENT_LAG = 2
-HEAD_VB = 32
-MID_VB = 26
-LAST_VB = [16, 16, 0, 8, 0]
+HEAD_SH = [(1, 2), (1, 2), (1, 2), (1, 2)]
+MID_SH = [(2, 2), (3, 2), (2, 3), (3, 2)]
+LAST_SH = [4, 2, 3, 3, 4, 4, 3, 4]
 Q_FIRST = 4
 
 
@@ -52,9 +53,10 @@ def tile_multiheadlatentattention_pb_kernel(tc, x, cos, sin, wq, out):
         ident = const.tile([P, P], F32, name="ident")
         cos_sb = const.tile([P, 64], BF16, name="cos_sb")
         sin_sb = const.tile([P, 64], BF16, name="sin_sb")
-        tab = const.tile([P, 2, 128], F32, name="tab")
+        tab = const.tile([P, 2, 512], F32, name="tab")
         warm = const.tile([P, 8], F32, name="warm")
         warm2 = const.tile([P, 8], F32, name="warm2")
+        idle = const.tile([P, 512], BF16, name="idle")
         xcodes = const.tile([P, NPASS, 512], U32, name="xcodes", align_bytes=64)
         xscales = const.tile([P, NPASS, 512], U8, name="xscales", align_bytes=64)
 
@@ -100,26 +102,31 @@ def tile_multiheadlatentattention_pb_kernel(tc, x, cos, sin, wq, out):
         def x_quant(g):
             nc.vector.quantize_mx(out=xcodes[:, g, :].bitcast(E5X4), scales=xscales[:, g, :], in_=xg[g][:])
 
-        def il(copy, u, lo, hi):
-            if lo >= hi:
-                return
+        def il(copy, u, lo, hi, even):
             G, kind, g = u
             dst = grp[u].rearrange("p (h b i j) -> p h b j i", h=4, i=4, j=4)
             for t, h0, nh in raw[(G, g)]:
+                a, b = max(lo, h0), min(hi, h0 + nh)
+                if a >= b:
+                    continue
                 src = t[:].rearrange("p j (h k b i) -> p k h b j i", k=2, b=32, i=4)[:, kind]
-                copy(out=dst[:, h0 : h0 + nh, lo:hi], in_=src[:, :, lo:hi])
+                cuts = [(a, b)]
+                if even and b - a == 3:
+                    cuts = [(a, a + 2), (a + 2, b)]
+                for c0, c1 in cuts:
+                    copy(out=dst[:, c0:c1], in_=src[:, c0 - h0 : c1 - h0])
 
-        def il_scalar(units, vb):
+        def il_scalar(units, heads):
             t = grpp.tile([P, 2, 2048], BF16, name="grp", align_bytes=64)
             for i in range(len(units)):
                 grp[units[i]] = t[:, i, :]
             grp[tuple(units)] = t
-            for u in units[:-1]:
-                il(nc.scalar.copy, u, 0, 32)
-            il(nc.scalar.copy, units[-1], vb, 32)
+            for i in range(len(units)):
+                il(nc.scalar.copy, units[i], 0, heads[i], False)
 
-        def il_vector(units, vb):
-            il(nc.vector.tensor_copy, units[-1], 0, vb)
+        def il_vector(units, heads):
+            for i in range(len(units)):
+                il(nc.vector.tensor_copy, units[i], heads[i], 4, True)
 
         def quant(units):
             n = len(units)
@@ -171,9 +178,9 @@ def tile_multiheadlatentattention_pb_kernel(tc, x, cos, sin, wq, out):
                 t = k4p.tile([P, 2, 512], F32, name="k4", align_bytes=64)
                 prod[m] = t
                 nc.vector.tensor_tensor(
-                    out=t[:].rearrange("p o (h q e) -> p o h q e", h=4, e=2),
-                    in0=tab[:].rearrange("p o (z q e) -> p o z q e", z=1, e=2).to_broadcast([P, 2, 4, 64, 2]),
-                    in1=a[:].rearrange("p (h q o z) -> p o h q z", h=4, o=2, z=1).to_broadcast([P, 2, 4, 64, 2]),
+                    out=t[:].rearrange("p o (q e) -> p o q e", e=2),
+                    in0=tab[:].rearrange("p o (q e) -> p o q e", e=2),
+                    in1=a[:].rearrange("p (q o z) -> p o q z", o=2, z=1).to_broadcast([P, 2, 256, 2]),
                     op=ALU.mult,
                 )
 
@@ -205,14 +212,16 @@ def tile_multiheadlatentattention_pb_kernel(tc, x, cos, sin, wq, out):
         SECOND = [CONTENT, CONTENT, CONTENT, CONTENT]
 
         nc.vector.memset(warm[:], 0.0)
+        nc.gpsimd.memset(idle[:], 0.0)
         nc.scalar.copy(out=warm2[:], in_=warm[:])
         make_identity(nc, ident[:])
         slots = RAWBUFS
         nxt = 0
-        nc.sync.dma_start(out=cos_sb[:], in_=cos)
-        nc.sync.dma_start(out=sin_sb[:], in_=sin)
         for s in range(NPASS):
             load_raw(s)
+            if s == 0:
+                nc.sync.dma_start(out=cos_sb[:], in_=cos)
+                nc.sync.dma_start(out=sin_sb[:], in_=sin)
             load_x(s)
             slots -= CHUNKS if s == 0 else 1
             nxt += 1
@@ -223,23 +232,24 @@ def tile_multiheadlatentattention_pb_kernel(tc, x, cos, sin, wq, out):
         next_raw = [nxt]
 
         def build_tables():
-            tv = tab[:].rearrange("p t (j e) -> p t j e", e=2)
-            for e in range(2):
-                nc.scalar.copy(out=tv[:, e, :, e], in_=cos_sb[:])
-                nc.scalar.mul(out=tv[:, e, :, 1 - e], in_=sin_sb[:], mul=(1.0 if e == 0 else -1.0))
+            tv = tab[:].rearrange("p t (h j e) -> p t h j e", h=4, e=2)
+            for h in range(4):
+                for e in range(2):
+                    nc.vector.tensor_copy(out=tv[:, e, h, :, e], in_=cos_sb[:])
+                    nc.vector.tensor_scalar_mul(out=tv[:, e, h, :, 1 - e], in0=sin_sb[:], scalar1=(1.0 if e == 0 else -1.0))
 
-        build_tables()
         steps = []
         for G in range(GROUPS - 1):
             for g in range(NPASS):
                 s = NPASS * G + g
-                steps.append(([(G, CONTENT, g), (G, ROPE, g)], HEAD_VB if s < NPASS else MID_VB))
+                sh = HEAD_SH[s] if s < len(HEAD_SH) else MID_SH[s % len(MID_SH)]
+                steps.append(([(G, ROPE, g), (G, CONTENT, g)], [sh[0], sh[1]]))
         G = GROUPS - 1
         last = [(G, ROPE, g) for g in range(NPASS)] + [(G, CONTENT, g) for g in range(NPASS)]
-        for i in range(3):
-            steps.append(([last[2 * i], last[2 * i + 1]], LAST_VB[i]))
-        steps.append(([last[6]], LAST_VB[3]))
-        steps.append(([last[7]], LAST_VB[4]))
+        for i in range(0, 6, 2):
+            steps.append(([last[i], last[i + 1]], [LAST_SH[i], LAST_SH[i + 1]]))
+        steps.append(([last[6]], [LAST_SH[6]]))
+        steps.append(([last[7]], [LAST_SH[7]]))
 
         uses = {}
         pending = []
@@ -293,6 +303,8 @@ def tile_multiheadlatentattention_pb_kernel(tc, x, cos, sin, wq, out):
             if 0 <= t < n:
                 il_vector(steps[t][0], steps[t][1])
                 free_raw(steps[t][0])
+            if t == 0:
+                build_tables()
             if 1 <= t <= NPASS:
                 x_quant(t - 1)
                 xq_done.add(t - 1)
@@ -311,6 +323,10 @@ def tile_multiheadlatentattention_pb_kernel(tc, x, cos, sin, wq, out):
                 else:
                     content(job[2])
             write_passes(t)
+            if t == n - 2:
+                spare = bank(4, [P, 512])
+                for i in range(KEEP_WARM):
+                    nc.tensor.matmul(out=spare[:], lhsT=idle[:, 0:P], rhs=idle[:], start=True, stop=True)
             a = t + 1
             if 0 <= a < n:
                 il_scalar(steps[a][0], steps[a][1])

from contextlib import ExitStack

import concourse.mybir as mybir
from concourse.masks import make_identity

F32 = mybir.dt.float32
BF16 = mybir.dt.bfloat16
U32 = mybir.dt.uint32
U8 = mybir.dt.uint8
E5X4 = mybir.dt.float8_e5m2_x4
ALU = mybir.AluOpType

P = 128
TOKENS, E, NOUT = 512, 2048, 4096
FLOPS = 2 * TOKENS * E * NOUT
NPASS = 4
MT = 4
GROUPS = 4
GW = 1024
ROPE, CONTENT = 1, 0

RAWBUFS = 8
GRPBUFS = 3
WCBUFS = 6
OTBUFS = 10
K4BUFS = 8
G_ADDS = 3
CHUNKS = 4
KEEP_WARM = 8
ROPE_LAG = 1
CONTENT_LAG = 2
HEAD_SH = [(1, 2), (1, 2), (1, 2), (1, 2)]
MID_SH = [(2, 2), (3, 2), (2, 3), (3, 2)]
LAST_SH = [4, 2, 3, 3, 4, 4, 3, 4]
Q_FIRST = 4


def tile_multiheadlatentattention_pb_kernel(tc, x, cos, sin, wq, out):
    nc = tc.nc
    x_rows = x.flatten_outer_dims()
    out_rows = out.rearrange("b l h d -> (b l) (h d)")

    with ExitStack() as ctx:
        const = ctx.enter_context(tc.tile_pool(name="const", bufs=1))
        rawp = ctx.enter_context(tc.tile_pool(name="rawp", bufs=RAWBUFS))
        k4p = ctx.enter_context(tc.tile_pool(name="k4p", bufs=K4BUFS))
        grpp = ctx.enter_context(tc.tile_pool(name="grpp", bufs=GRPBUFS))
        wcp = ctx.enter_context(tc.tile_pool(name="wcp", bufs=WCBUFS))
        otp = ctx.enter_context(tc.tile_pool(name="otp", bufs=OTBUFS))
        psum = ctx.enter_context(tc.psum_pool(name="psum", bufs=1))
        ctx.enter_context(tc.manual_schedule())

        ident = const.tile([P, P], F32, name="ident")
        cos_sb = const.tile([P, 64], BF16, name="cos_sb")
        sin_sb = const.tile([P, 64], BF16, name="sin_sb")
        tab = const.tile([P, 2, 512], F32, name="tab")
        warm = const.tile([P, 8], F32, name="warm")
        warm2 = const.tile([P, 8], F32, name="warm2")
        idle = const.tile([P, 512], BF16, name="idle")
        xcodes = const.tile([P, NPASS, 512], U32, name="xcodes", align_bytes=64)
        xscales = const.tile([P, NPASS, 512], U8, name="xscales", align_bytes=64)

        raw, xk, xg, grp, wcodes, wscales, acc, ot = {}, {}, {}, {}, {}, {}, {}, {}

        def bank(i, shape):
            return psum.tile(shape, F32, name="bank%d" % i)

        def load_raw(s):
            G, g = s // NPASS, s % NPASS
            nch = CHUNKS if s == 0 else 1
            nh = 4 // nch
            pieces = []
            for c in range(nch):
                t = rawp.tile([P, 4, 256 * nh], BF16, name="raw")
                pieces.append((t, nh * c, nh))
                nc.sync.dma_start(
                    out=t[:],
                    in_=wq[512 * g : 512 * (g + 1), GW * G + 256 * nh * c : GW * G + 256 * nh * (c + 1)].rearrange("(p j) w -> p j w", j=4),
                )
            raw[(G, g)] = pieces

        def load_x(g):
            t = k4p.tile([P, MT, 512], BF16, name="k4", align_bytes=64)
            xk[g] = t
            nc.sync.dma_start(out=t[:], in_=x_rows[:, 512 * g : 512 * (g + 1)].rearrange("(m p) k -> p m k", p=P))

        def x_turn(g):
            words = xk[g][:].bitcast(F32)
            t = k4p.tile([P, E], BF16, name="k4", align_bytes=64)
            xg[g] = t
            xgw = t[:].bitcast(F32).rearrange("p (m r u) -> p m r u", m=MT, u=2)
            for half in range(2):
                tp = bank(2 * (g % 2) + half, [P, 4, P])
                for mm in range(2):
                    for u in range(2):
                        nc.tensor.transpose(tp[:, 2 * mm + u, :], words[:, 2 * half + mm, u : 256 : 2], ident[:])
                nc.scalar.copy(
                    out=xgw[:, 2 * half : 2 * half + 2],
                    in_=tp[:].rearrange("p (m u) r -> p m r u", u=2),
                )

        def x_quant(g):
            nc.vector.quantize_mx(out=xcodes[:, g, :].bitcast(E5X4), scales=xscales[:, g, :], in_=xg[g][:])

        def il(copy, u, lo, hi, even):
            G, kind, g = u
            dst = grp[u].rearrange("p (h b i j) -> p h b j i", h=4, i=4, j=4)
            for t, h0, nh in raw[(G, g)]:
                a, b = max(lo, h0), min(hi, h0 + nh)
                if a >= b:
                    continue
                src = t[:].rearrange("p j (h k b i) -> p k h b j i", k=2, b=32, i=4)[:, kind]
                cuts = [(a, b)]
                if even and b - a == 3:
                    cuts = [(a, a + 2), (a + 2, b)]
                for c0, c1 in cuts:
                    copy(out=dst[:, c0:c1], in_=src[:, c0 - h0 : c1 - h0])

        def il_scalar(units, heads):
            t = grpp.tile([P, 2, 2048], BF16, name="grp", align_bytes=64)
            for i in range(len(units)):
                grp[units[i]] = t[:, i, :]
            grp[tuple(units)] = t
            for i in range(len(units)):
                il(nc.scalar.copy, units[i], 0, heads[i], False)

        def il_vector(units, heads):
            for i in range(len(units)):
                il(nc.vector.tensor_copy, units[i], heads[i], 4, True)

        def quant(units):
            n = len(units)
            c = wcp.tile([P, 2, 512], U32, name="wc", align_bytes=64)
            s = wcp.tile([P, 2, 512], U8, name="ws", align_bytes=64)
            for i in range(n):
                wcodes[units[i]], wscales[units[i]] = c[:, i, :], s[:, i, :]
            t = grp[tuple(units)]
            nc.vector.quantize_mx(
                out=c[:, 0:n, :].rearrange("p a w -> p (a w)").bitcast(E5X4),
                scales=s[:, 0:n, :].rearrange("p a w -> p (a w)"),
                in_=t[:, 0:n, :].rearrange("p a w -> p (a w)"),
            )

        def one_pass(u, m):
            G, kind, g = u
            if g == 0:
                acc[(G, kind, m)] = bank(4 * kind + m, [P, 512])
            nc.tensor.matmul_mx(
                out=acc[(G, kind, m)][:],
                lhsT=xcodes[:, g, P * m : P * (m + 1)].bitcast(E5X4),
                lhsT_scale=xscales[:, g, P * m : P * (m + 1)],
                rhs=wcodes[u].bitcast(E5X4),
                rhs_scale=wscales[u],
                start=(g == 0),
                stop=(g == NPASS - 1),
            )

        def ot_tile(G, m):
            if (G, m) not in ot:
                ot[(G, m)] = otp.tile([P, GW], F32, name="ot")
            return ot[(G, m)]

        def ot_part(G, m, kind):
            return ot_tile(G, m)[:].rearrange("p (h k c) -> p k h c", k=2, c=128)[:, kind]

        def store(G, m, kind):
            rows = out_rows[P * m : P * (m + 1), GW * G : GW * (G + 1)]
            if G == GROUPS - 1:
                nc.sync.dma_start(out=rows.rearrange("p (h k c) -> p k h c", k=2, c=128)[:, kind], in_=ot_part(G, m, kind))
            elif kind == SECOND[G]:
                nc.sync.dma_start(out=rows, in_=ot_tile(G, m)[:])

        def rope(G):
            prod = {}

            def mul(m):
                a = acc[(G, ROPE, m)]
                t = k4p.tile([P, 2, 512], F32, name="k4", align_bytes=64)
                prod[m] = t
                nc.vector.tensor_tensor(
                    out=t[:].rearrange("p o (q e) -> p o q e", e=2),
                    in0=tab[:].rearrange("p o (q e) -> p o q e", e=2),
                    in1=a[:].rearrange("p (q o z) -> p o q z", o=2, z=1).to_broadcast([P, 2, 256, 2]),
                    op=ALU.mult,
                )

            def add(m):
                eng = nc.gpsimd if m < G_ADDS else nc.vector
                eng.tensor_tensor(
                    out=ot_part(G, m, ROPE),
                    in0=prod[m][:, 0, :].rearrange("p (h c) -> p h c", c=128),
                    in1=prod[m][:, 1, :].rearrange("p (h c) -> p h c", c=128),
                    op=ALU.add,
                )
                store(G, m, ROPE)

            mul(0)
            for m in range(1, MT):
                mul(m)
                add(m - 1)
            return lambda: add(MT - 1)

        def content(G):
            for m in range(MT):
                src = acc[(G, CONTENT, m)][:].rearrange("p (h c) -> p h c", c=128)
                if G == GROUPS - 1 and m % 2 == 1:
                    nc.vector.tensor_copy(out=ot_part(G, m, CONTENT), in_=src)
                else:
                    nc.scalar.copy(out=ot_part(G, m, CONTENT), in_=src)
                store(G, m, CONTENT)

        SECOND = [CONTENT, CONTENT, CONTENT, CONTENT]

        nc.vector.memset(warm[:], 0.0)
        nc.gpsimd.memset(idle[:], 0.0)
        nc.scalar.copy(out=warm2[:], in_=warm[:])
        make_identity(nc, ident[:])
        slots = RAWBUFS
        nxt = 0
        for s in range(NPASS):
            load_raw(s)
            if s == 0:
                nc.sync.dma_start(out=cos_sb[:], in_=cos)
                nc.sync.dma_start(out=sin_sb[:], in_=sin)
            load_x(s)
            slots -= CHUNKS if s == 0 else 1
            nxt += 1
        while slots > 0:
            load_raw(nxt)
            nxt += 1
            slots -= 1
        next_raw = [nxt]

        def build_tables():
            tv = tab[:].rearrange("p t (h j e) -> p t h j e", h=4, e=2)
            for h in range(4):
                for e in range(2):
                    nc.vector.tensor_copy(out=tv[:, e, h, :, e], in_=cos_sb[:])
                    nc.vector.tensor_scalar_mul(out=tv[:, e, h, :, 1 - e], in0=sin_sb[:], scalar1=(1.0 if e == 0 else -1.0))

        steps = []
        for G in range(GROUPS - 1):
            for g in range(NPASS):
                s = NPASS * G + g
                sh = HEAD_SH[s] if s < len(HEAD_SH) else MID_SH[s % len(MID_SH)]
                steps.append(([(G, ROPE, g), (G, CONTENT, g)], [sh[0], sh[1]]))
        G = GROUPS - 1
        last = [(G, ROPE, g) for g in range(NPASS)] + [(G, CONTENT, g) for g in range(NPASS)]
        for i in range(0, 6, 2):
            steps.append(([last[i], last[i + 1]], [LAST_SH[i], LAST_SH[i + 1]]))
        steps.append(([last[6]], [LAST_SH[6]]))
        steps.append(([last[7]], [LAST_SH[7]]))

        uses = {}
        pending = []
        done = set()
        queues = {ROPE: [], CONTENT: []}
        late_adds = []
        n = len(steps)

        def free_raw(units):
            for u in units:
                key = (u[0], u[2])
                uses[key] = uses.get(key, 0) + 1
                if uses[key] == 2:
                    for i in range(len(raw[key])):
                        if next_raw[0] < GROUPS * NPASS:
                            load_raw(next_raw[0])
                            next_raw[0] += 1

        def write_passes(t):
            for kind in (ROPE, CONTENT):
                q = queues[kind]
                if kind == CONTENT and len(q) > 0 and q[0][0] == 0:
                    if len(q) < NPASS or q[NPASS - 1][0] != 0 or len(xq_done) < NPASS:
                        continue
                    for m in range(MT):
                        for g in range(NPASS):
                            one_pass(q[g], m)
                    for g in range(NPASS):
                        q.pop(0)
                    pending.append((t + CONTENT_LAG, CONTENT, 0))
                while len(q) > 0:
                    u = q[0]
                    if u[2] == 0 and u[0] > 0 and (u[0] - 1, kind) not in done:
                        break
                    if u[0] == 0 and u[2] not in xq_done:
                        break
                    for m in range(MT):
                        one_pass(u, m)
                    q.pop(0)
                    if u[2] == NPASS - 1:
                        pending.append((t + (ROPE_LAG if kind == ROPE else CONTENT_LAG), kind, u[0]))

        xq_done = set()

        def do_quant(s):
            quant(steps[s][0])
            for u in steps[s][0]:
                queues[u[1]].append(u)

        for t in range(-1, n + 5):
            if 0 <= t < n:
                il_vector(steps[t][0], steps[t][1])
                free_raw(steps[t][0])
            if t == 0:
                build_tables()
            if 1 <= t <= NPASS:
                x_quant(t - 1)
                xq_done.add(t - 1)
            if 0 <= t < NPASS:
                do_quant(t)
            if NPASS < t <= n:
                do_quant(t - 1)
            for last_add in late_adds:
                last_add()
            late_adds.clear()
            for job in [j for j in pending if j[0] <= t]:
                pending.remove(job)
                done.add((job[2], job[1]))
                if job[1] == ROPE:
                    late_adds.append(rope(job[2]))
                else:
                    content(job[2])
            write_passes(t)
            if t == n - 2:
                spare = bank(4, [P, 512])
                for i in range(KEEP_WARM):
                    nc.tensor.matmul(out=spare[:], lhsT=idle[:, 0:P], rhs=idle[:], start=True, stop=True)
            a = t + 1
            if 0 <= a < n:
                il_scalar(steps[a][0], steps[a][1])
            if 0 <= a < NPASS:
                x_turn(a)
